import numpy as np
import ml_dtypes


def mxq(x, axis, fmt="e4m3"):
    dtype, down = {"e4m3": (ml_dtypes.float8_e4m3fn, 7), "e5m2": (ml_dtypes.float8_e5m2, 14)}[fmt]
    v = np.moveaxis(np.asarray(x, np.float32).astype(ml_dtypes.bfloat16).astype(np.float64), axis, -1)
    blocks = v.reshape(v.shape[:-1] + (-1, 32))
    amax = np.abs(blocks).max(-1, keepdims=True)
    byte = np.maximum(np.where(amax > 0, np.frexp(amax)[1] - 1 + 127, 0) - down, 1)
    scale = np.exp2(byte - 127.0)
    codes = (blocks / scale).astype(np.float32).astype(dtype).astype(np.float64)
    return np.moveaxis((codes * scale).reshape(v.shape), -1, axis)


WIDE = False


def mx_kscale(k):
    if not WIDE:
        return np.ones(k)
    levels = np.array([10, -10, 5, -5, 0])
    a = np.random.permutation(np.resize(levels, k // 512 * 4)).reshape(k // 512, 4)
    idx = np.arange(k)
    return np.exp2(a[idx // 512, idx % 128 // 32])


BF16 = ml_dtypes.bfloat16


def bf(x):
    return np.asarray(x, np.float32).astype(BF16)


def f64(x):
    return np.asarray(x).astype(np.float64)


E2M1 = np.array([0.0, 0.5, 1.0, 1.5, 2.0, 3.0, 4.0, 6.0, -0.0, -0.5, -1.0, -1.5, -2.0, -3.0, -4.0, -6.0])


def pack_weight(w, fmt):
    k, n = w.shape
    w = f64(bf(w)).reshape(k // 32, 32, n)
    amax = np.abs(w).max(1)
    if fmt == "e4m3":
        byte = np.frexp(amax)[1] - 1 + 127 - 7
    else:
        mant, ex = np.frexp(amax / 6.0)
        byte = np.where(mant > 0.5, ex, ex - 1) + 127
    byte = np.clip(np.where(amax > 0, byte, 1), 1, 254)
    scaled = (w * np.exp2(127.0 - byte)[:, None, :]).reshape(k, n).astype(np.float32)
    by_word = np.ascontiguousarray(scaled.reshape(k // 512, 128, 4, n).transpose(0, 1, 3, 2))
    if fmt == "e4m3":
        words = by_word.astype(ml_dtypes.float8_e4m3fn).view(np.uint8)
    else:
        c = by_word.astype(ml_dtypes.float4_e2m1fn).view(np.uint8) & 0xF
        words = c[..., 0::2] | (c[..., 1::2] << 4)
    return np.ascontiguousarray(words), np.ascontiguousarray(byte.astype(np.uint8).reshape(k // 512, 16, n))


def unpack_weight(words, scales, fmt):
    g, p, n, _ = words.shape
    if fmt == "e4m3":
        vals = np.ascontiguousarray(words).view(ml_dtypes.float8_e4m3fn).astype(np.float64)
    else:
        nib = np.empty((g, p, n, 4), np.uint8)
        nib[..., 0::2] = words & 0xF
        nib[..., 1::2] = words >> 4
        vals = E2M1[nib]
    vals = vals * np.repeat(np.exp2(scales.astype(np.float64) - 127.0), 8, axis=1)[..., None]
    return vals.transpose(0, 1, 3, 2).reshape(g * 512, n)


B, C, P, NH, NW = 4, 4, 16, 16, 16
D = C * P * P
QK_SCALE = 1.0
FMT = "e4m3"


def rel_bias(p):
    i = np.arange(p, dtype=np.float64)
    down = np.exp(-i / (p / 2))[:, None] * np.ones((1, p))
    right = down.T
    br = np.exp(-(i[:, None] + i[None, :]) / (p / 2))
    return np.stack([
        np.rot90(br, 2), np.flip(down, 0), np.rot90(br, 1),
        np.flip(right, 1), np.ones((p, p)), right,
        np.rot90(br, 3), down, br,
    ], axis=0)


def setup_inputs():
    s = mx_kscale(D)
    sx = np.tile(s.reshape(C, P, P), (1, NH, NW))
    x = bf(np.random.standard_normal((B, C, NH * P, NW * P)) * sx)
    w = np.random.standard_normal((3 * D, D)) / np.sqrt(D) / s
    words, scales = pack_weight(np.ascontiguousarray(w.T), FMT)
    b_qkv = bf(np.random.standard_normal(3 * D) * 0.5)
    return {"x": x,
            "W_qkv_words": words,
            "W_qkv_scales": scales,
            "b_qkv": b_qkv}


def reference(x, W_qkv_words, W_qkv_scales, b_qkv):
    p, c = P, C
    b, _, h, w = x.shape
    nh, nw = h // p, w // p
    feat = f64(x).reshape(b, c, nh, p, nw, p).transpose(0, 2, 4, 1, 3, 5).reshape(b, nh, nw, c * p * p)
    y = mxq(feat, 3, "e4m3") @ unpack_weight(W_qkv_words, W_qkv_scales, FMT)
    qkv = np.pad(y, ((0, 0), (1, 1), (1, 1), (0, 0))) + f64(b_qkv)
    qkv = qkv.reshape(b, nh + 2, nw + 2, 3, c, p, p)
    core_q = qkv[:, 1:nh + 1, 1:nw + 1, 0] * QK_SCALE
    k = np.stack([qkv[:, di:di + nh, dj:dj + nw, 1] for di in range(3) for dj in range(3)], axis=3)
    v = np.stack([qkv[:, di:di + nh, dj:dj + nw, 2] for di in range(3) for dj in range(3)], axis=3)
    bias = rel_bias(p)
    attn = core_q[:, :, :, None] * k * bias[:, None]
    out = np.sum(attn * v, axis=3)
    return out.transpose(0, 3, 1, 4, 2, 5).reshape(b, c, nh * p, nw * p)

@@ -1,0 +1,245 @@
+from contextlib import ExitStack
+
+import concourse.mybir as mybir
+from concourse.masks import make_identity
+
+F32 = mybir.dt.float32
+BF16 = mybir.dt.bfloat16
+I32 = mybir.dt.int32
+U32 = mybir.dt.uint32
+U8 = mybir.dt.uint8
+FP8X4 = mybir.dt.float8_e4m3fn_x4
+ALU = mybir.AluOpType
+ACT = mybir.ActivationFunctionType
+
+P = 128
+BATCH = 4
+CHANNELS = 4
+PATCH = 16
+GRID = 16
+WIDTH = GRID * PATCH
+D = CHANNELS * PATCH * PATCH
+PATCHES = BATCH * GRID * GRID
+K_PASS = 4 * P
+PASSES = D // K_PASS
+BANK = 512
+HALVES = PATCHES // BANK
+COLUMN = GRID * BATCH
+J_BANK = BANK // COLUMN
+E_TILES = D // P
+PAD = 8
+
+FLOPS = 2 * PATCHES * D * 3 * D
+
+
+def tile_attentionconv_kernel(tc, x, W_qkv_words, W_qkv_scales, b_qkv, out):
+    nc = tc.nc
+    with ExitStack() as ctx:
+        keep = ctx.enter_context(tc.tile_pool(name="keep", bufs=1))
+        work = ctx.enter_context(tc.tile_pool(name="work", bufs=2))
+        psum = ctx.enter_context(tc.psum_pool(name="psum", bufs=6))
+        psum_t = ctx.enter_context(tc.psum_pool(name="psum_t", bufs=2))
+
+        x_rows = x.rearrange("b (g c) (i r) w -> c i (b g) (r w)", g=2, c=2, i=GRID, r=PATCH)
+        x_sb = keep.tile([P, 2, PATCH * WIDTH], BF16)
+        for c in range(2):
+            nc.sync.dma_start(out=x_sb[:, c, :], in_=x_rows[c])
+
+        bias_rows = keep.tile([P, P], BF16)
+        nc.vector.memset(bias_rows[:], 0.0)
+        nc.sync.dma_start(out=bias_rows[0 : 3 * E_TILES, :], in_=b_qkv.rearrange("(t p) -> t p", p=P))
+
+        w_scales = keep.tile([P, PASSES, 3 * D], U8, align_bytes=64)
+        nc.vector.memset(w_scales[:].rearrange("p g n -> p (g n)").bitcast(I32), 0)
+        for quad in range(4):
+            nc.sync.dma_start(
+                out=w_scales[32 * quad : 32 * quad + 4, :, :].bitcast(I32),
+                in_=W_qkv_scales[:, 4 * quad : 4 * quad + 4, :].rearrange("g r n -> r g n").bitcast(I32),
+            )
+
+        w_words = keep.tile([P, PASSES, 3 * D], U32, align_bytes=64)
+        for section in (1, 2, 0):
+            for g in range(PASSES):
+                nc.sync.dma_start(
+                    out=w_words[:, g, section * D : (section + 1) * D].bitcast(I32),
+                    in_=W_qkv_words[g]
+                    .rearrange("p n t -> p (n t)")[:, 4 * section * D : 4 * (section + 1) * D]
+                    .bitcast(I32),
+                )
+
+        ident = keep.tile([P, P], F32)
+        make_identity(nc, ident[:])
+
+        p_index = keep.tile([P, 1], I32)
+        nc.gpsimd.iota(p_index[:], pattern=[[0, 1]], base=0, channel_multiplier=1)
+        rs_int = keep.tile([P, 2], I32)
+        nc.vector.tensor_single_scalar(out=rs_int[:, 0:1], in_=p_index[:], scalar=PATCH - 1, op=ALU.bitwise_and)
+        nc.vector.tensor_single_scalar(out=rs_int[:, 1:2], in_=p_index[:], scalar=4, op=ALU.logical_shift_right)
+        rs = keep.tile([P, 2], F32)
+        nc.vector.tensor_copy(out=rs[:], in_=rs_int[:])
+        s_col = rs[:, 0:1]
+        r_col = rs[:, 1:2]
+        exponents = keep.tile([P, 6], F32)
+        nc.vector.tensor_scalar(out=exponents[:, 0:1], in0=s_col, scalar1=0.125, scalar2=-15.0 / 8.0, op0=ALU.mult, op1=ALU.add)
+        nc.vector.tensor_scalar(out=exponents[:, 1:2], in0=s_col, scalar1=-0.125, scalar2=0.0, op0=ALU.mult, op1=ALU.add)
+        for upper in range(2):
+            nc.vector.tensor_scalar(out=exponents[:, 2 + upper : 3 + upper], in0=r_col, scalar1=0.125, scalar2=(8.0 * upper - 15.0) / 8.0, op0=ALU.mult, op1=ALU.add)
+            nc.vector.tensor_scalar(out=exponents[:, 4 + upper : 5 + upper], in0=r_col, scalar1=-0.125, scalar2=-1.0 * upper, op0=ALU.mult, op1=ALU.add)
+        taps = keep.tile([P, 6], F32)
+        nc.scalar.activation(out=taps[:], in_=exponents[:], func=ACT.Exp)
+
+        bias_rows_f32 = keep.tile([P, P], F32)
+        nc.vector.tensor_copy(out=bias_rows_f32[:], in_=bias_rows[:])
+        bias_t = psum_t.tile([P, 4, P], F32, tag="tr")
+        nc.tensor.transpose(bias_t[:, 0, :], bias_rows_f32[:], ident[:])
+        bias = keep.tile([P, 3 * E_TILES], F32)
+        nc.vector.tensor_copy(out=bias[:], in_=bias_t[:, 0, 0 : 3 * E_TILES])
+
+        edge = keep.tile([P, E_TILES], F32)
+        nc.vector.tensor_tensor(out=edge[:], in0=bias[:, E_TILES : 2 * E_TILES], in1=bias[:, 2 * E_TILES : 3 * E_TILES], op=ALU.mult)
+        tap_sum = keep.tile([P, 2], F32)
+        nc.vector.scalar_tensor_tensor(out=tap_sum[:], in0=taps[:, 2:4], scalar=1.0, in1=taps[:, 4:6], op0=ALU.add, op1=ALU.add)
+        edge_rows = keep.tile([P, E_TILES], F32)
+        nc.vector.tensor_tensor(
+            out=edge_rows[:].rearrange("p (c h) -> p c h", h=2),
+            in0=edge[:].rearrange("p (c h) -> p c h", h=2),
+            in1=tap_sum[:].unsqueeze(1).to_broadcast([P, CHANNELS, 2]),
+            op=ALU.mult,
+        )
+
+        x_words = (
+            x_sb[:]
+            .rearrange("p c e -> p (c e)")
+            .bitcast(F32)
+            .rearrange("p (cr j s u) -> p u j cr s", cr=2 * PATCH, j=GRID, s=4, u=2)
+        )
+        sorted_words = keep.tile([P, GRID, 2, P], F32)
+        grouped = keep.tile([P, PASSES, 4 * PATCHES], BF16, align_bytes=64)
+        grouped_words = grouped[:].bitcast(F32)
+        x_codes = keep.tile([P, PASSES, PATCHES], U32, align_bytes=64)
+        x_scales = keep.tile([P, PASSES, PATCHES], U8, align_bytes=64)
+        for half in range(HALVES):
+            for j0 in range(half * J_BANK, (half + 1) * J_BANK, 4):
+                for u in range(2):
+                    nc.vector.tensor_copy(
+                        out=sorted_words[:, j0 : j0 + 4, u, :].rearrange("p j (cr s) -> p j cr s", s=4),
+                        in_=x_words[:, u, j0 : j0 + 4],
+                    )
+            for j0 in range(half * J_BANK, (half + 1) * J_BANK, 2):
+                x_t = psum.tile([P, 4, P], F32, tag="acc")
+                for jl in range(2):
+                    for u in range(2):
+                        nc.tensor.transpose(x_t[:, 2 * jl + u, :], sorted_words[:, j0 + jl, u, :], ident[:])
+                by_pass = x_t[:].rearrange("p (jl u) (n g) -> p g jl n u", u=2, g=PASSES)
+                for g in range(PASSES):
+                    nc.scalar.copy(
+                        out=grouped_words[:, g, j0 * 2 * COLUMN : (j0 + 2) * 2 * COLUMN].rearrange(
+                            "p (jl n u) -> p jl n u", jl=2, u=2
+                        ),
+                        in_=by_pass[:, g],
+                    )
+            for g in range(PASSES):
+                nc.vector.quantize_mx(
+                    out=x_codes[:, g, half * BANK : (half + 1) * BANK].bitcast(FP8X4),
+                    scales=x_scales[:, g, half * BANK : (half + 1) * BANK],
+                    in_=grouped[:, g, 4 * half * BANK : 4 * (half + 1) * BANK],
+                )
+
+        def project(n_tile, half):
+            acc = psum.tile([P, BANK], F32, tag="acc")
+            features = slice(n_tile * P, (n_tile + 1) * P)
+            patches = slice(half * BANK, (half + 1) * BANK)
+            for g in range(PASSES):
+                nc.tensor.matmul_mx(
+                    out=acc[:],
+                    lhsT=w_words[:, g, features].bitcast(FP8X4),
+                    lhsT_scale=w_scales[:, g, features],
+                    rhs=x_codes[:, g, patches].bitcast(FP8X4),
+                    rhs_scale=x_scales[:, g, patches],
+                    start=(g == 0),
+                    stop=(g == PASSES - 1),
+                )
+            return acc
+
+        out_rows = out.rearrange("b c (m r) w -> c m b (r w)", r=PATCH // 2)
+        for channel in range(CHANNELS):
+            result = work.tile([P, GRID, GRID, 2, BATCH], F32)
+            for upper in range(2):
+                et = 2 * channel + upper
+                b_q = bias[:, et : et + 1]
+                b_k = bias[:, E_TILES + et : E_TILES + et + 1]
+                b_v = bias[:, 2 * E_TILES + et : 2 * E_TILES + et + 1]
+
+                k_sb = work.tile([P, PATCHES], F32)
+                kv_pad = work.tile([P, GRID, PAD + COLUMN + PAD], F32)
+                nc.scalar.copy(
+                    out=kv_pad[:].rearrange("p j (k w) -> p j k w", w=PAD)[:, :, 0 : COLUMN // PAD + 2 : COLUMN // PAD + 1, :],
+                    in_=edge[:, et : et + 1].unsqueeze(2).unsqueeze(3).to_broadcast([P, GRID, 2, PAD]),
+                )
+                for half in range(HALVES):
+                    k_ps = project(E_TILES + et, half)
+                    nc.scalar.activation(out=k_sb[:, half * BANK : (half + 1) * BANK], in_=k_ps[:], func=ACT.Identity, bias=b_k, scale=1.0)
+                for half in range(HALVES):
+                    v_ps = project(2 * E_TILES + et, half)
+                    nc.vector.scalar_tensor_tensor(
+                        out=kv_pad[:, half * J_BANK : (half + 1) * J_BANK, PAD : PAD + COLUMN],
+                        in0=v_ps[:].rearrange("p (j n) -> p j n", n=COLUMN),
+                        scalar=b_v,
+                        in1=k_sb[:, half * BANK : (half + 1) * BANK].rearrange("p (j n) -> p j n", n=COLUMN),
+                        op0=ALU.add,
+                        op1=ALU.mult,
+                    )
+
+                rows_pad = work.tile([P, GRID + 2, COLUMN], F32)
+                nc.scalar.copy(
+                    out=rows_pad[:, 0 : GRID + 2 : GRID + 1, :],
+                    in_=edge_rows[:, et : et + 1].unsqueeze(2).to_broadcast([P, 2, COLUMN]),
+                )
+                inner = rows_pad[:, 1 : GRID + 1, :]
+                nc.vector.scalar_tensor_tensor(
+                    out=inner,
+                    in0=kv_pad[:, :, PAD - BATCH : PAD - BATCH + COLUMN],
+                    scalar=taps[:, 2 + upper : 3 + upper],
+                    in1=kv_pad[:, :, PAD : PAD + COLUMN],
+                    op0=ALU.mult,
+                    op1=ALU.add,
+                )
+                nc.vector.scalar_tensor_tensor(
+                    out=inner,
+                    in0=kv_pad[:, :, PAD + BATCH : PAD + BATCH + COLUMN],
+                    scalar=taps[:, 4 + upper : 5 + upper],
+                    in1=inner,
+                    op0=ALU.mult,
+                    op1=ALU.add,
+                )
+
+                window = work.tile([P, GRID, COLUMN], F32)
+                nc.vector.scalar_tensor_tensor(
+                    out=window[:], in0=rows_pad[:, 0:GRID, :], scalar=taps[:, 0:1], in1=inner, op0=ALU.mult, op1=ALU.add
+                )
+                nc.vector.scalar_tensor_tensor(
+                    out=window[:], in0=rows_pad[:, 2 : GRID + 2, :], scalar=taps[:, 1:2], in1=window[:], op0=ALU.mult, op1=ALU.add
+                )
+
+                for half in range(HALVES):
+                    q_ps = project(et, half)
+                    js = slice(half * J_BANK, (half + 1) * J_BANK)
+                    nc.vector.scalar_tensor_tensor(
+                        out=result[:, js, :, upper, :],
+                        in0=q_ps[:].rearrange("p (j i b) -> p j i b", i=GRID, b=BATCH),
+                        scalar=b_q,
+                        in1=window[:, js, :].rearrange("p j (i b) -> p j i b", b=BATCH),
+                        op0=ALU.add,
+                        op1=ALU.mult,
+                    )
+
+            image_rows = work.tile([P, PATCH // 2, GRID, PATCH], F32)
+            for j0 in range(0, GRID, 4):
+                out_t = psum_t.tile([P, 4, P], F32, tag="tr")
+                for jl in range(4):
+                    nc.tensor.transpose(out_t[:, jl, :], result[:, j0 + jl].rearrange("p i h b -> p (i h b)"), ident[:])
+                nc.scalar.copy(
+                    out=image_rows[:, :, j0 : j0 + 4, :],
+                    in_=out_t[:].rearrange("p j (r s) -> p r j s", s=PATCH),
+                )
+            nc.sync.dma_start(out=out_rows[channel], in_=image_rows[:].rearrange("p r j s -> p (r j s)"))

@@ -35,10 +35,10 @@ FLOPS = 2 * PATCHES * D * 3 * D
 def tile_attentionconv_kernel(tc, x, W_qkv_words, W_qkv_scales, b_qkv, out):
     nc = tc.nc
     with ExitStack() as ctx:
+        ctx.enter_context(tc.manual_schedule())
         keep = ctx.enter_context(tc.tile_pool(name="keep", bufs=1))
         work = ctx.enter_context(tc.tile_pool(name="work", bufs=2))
-        psum = ctx.enter_context(tc.psum_pool(name="psum", bufs=6))
-        psum_t = ctx.enter_context(tc.psum_pool(name="psum_t", bufs=2))
+        psum = ctx.enter_context(tc.psum_pool(name="psum", bufs=4))
 
         x_rows = x.rearrange("b (g c) (i r) w -> c i (b g) (r w)", g=2, c=2, i=GRID, r=PATCH)
         x_sb = keep.tile([P, 2, PATCH * WIDTH], BF16)
@@ -47,7 +47,7 @@ def tile_attentionconv_kernel(tc, x, W_qkv_words, W_qkv_scales, b_qkv, out):
 
         bias_rows = keep.tile([P, P], BF16)
         nc.vector.memset(bias_rows[:], 0.0)
-        nc.sync.dma_start(out=bias_rows[0 : 3 * E_TILES, :], in_=b_qkv.rearrange("(t p) -> t p", p=P))
+        nc.scalar.dma_start(out=bias_rows[0 : 3 * E_TILES, :], in_=b_qkv.rearrange("(t p) -> t p", p=P))
 
         w_scales = keep.tile([P, PASSES, 3 * D], U8, align_bytes=64)
         nc.vector.memset(w_scales[:].rearrange("p g n -> p (g n)").bitcast(I32), 0)
@@ -90,10 +90,10 @@ def tile_attentionconv_kernel(tc, x, W_qkv_words, W_qkv_scales, b_qkv, out):
 
         bias_rows_f32 = keep.tile([P, P], F32)
         nc.vector.tensor_copy(out=bias_rows_f32[:], in_=bias_rows[:])
-        bias_t = psum_t.tile([P, 4, P], F32, tag="tr")
-        nc.tensor.transpose(bias_t[:, 0, :], bias_rows_f32[:], ident[:])
+        bias_t = psum.tile([P, BANK], F32, tag="kq")
+        nc.tensor.transpose(bias_t[:, 0:P], bias_rows_f32[:], ident[:])
         bias = keep.tile([P, 3 * E_TILES], F32)
-        nc.vector.tensor_copy(out=bias[:], in_=bias_t[:, 0, 0 : 3 * E_TILES])
+        nc.vector.tensor_copy(out=bias[:], in_=bias_t[:, 0 : 3 * E_TILES])
 
         edge = keep.tile([P, E_TILES], F32)
         nc.vector.tensor_tensor(out=edge[:], in0=bias[:, E_TILES : 2 * E_TILES], in1=bias[:, 2 * E_TILES : 3 * E_TILES], op=ALU.mult)
@@ -114,30 +114,29 @@ def tile_attentionconv_kernel(tc, x, W_qkv_words, W_qkv_scales, b_qkv, out):
             .rearrange("p (cr j s u) -> p u j cr s", cr=2 * PATCH, j=GRID, s=4, u=2)
         )
         sorted_words = keep.tile([P, GRID, 2, P], F32)
+        for j0 in range(0, GRID, 4):
+            for u in range(2):
+                nc.vector.tensor_copy(
+                    out=sorted_words[:, j0 : j0 + 4, u, :].rearrange("p j (cr s) -> p j cr s", s=4),
+                    in_=x_words[:, u, j0 : j0 + 4],
+                )
+
         grouped = keep.tile([P, PASSES, 4 * PATCHES], BF16, align_bytes=64)
         grouped_words = grouped[:].bitcast(F32)
         x_codes = keep.tile([P, PASSES, PATCHES], U32, align_bytes=64)
         x_scales = keep.tile([P, PASSES, PATCHES], U8, align_bytes=64)
         for half in range(HALVES):
-            for j0 in range(half * J_BANK, (half + 1) * J_BANK, 4):
-                for u in range(2):
-                    nc.vector.tensor_copy(
-                        out=sorted_words[:, j0 : j0 + 4, u, :].rearrange("p j (cr s) -> p j cr s", s=4),
-                        in_=x_words[:, u, j0 : j0 + 4],
-                    )
             for j0 in range(half * J_BANK, (half + 1) * J_BANK, 2):
-                x_t = psum.tile([P, 4, P], F32, tag="acc")
-                for jl in range(2):
-                    for u in range(2):
-                        nc.tensor.transpose(x_t[:, 2 * jl + u, :], sorted_words[:, j0 + jl, u, :], ident[:])
-                by_pass = x_t[:].rearrange("p (jl u) (n g) -> p g jl n u", u=2, g=PASSES)
-                for g in range(PASSES):
-                    nc.scalar.copy(
-                        out=grouped_words[:, g, j0 * 2 * COLUMN : (j0 + 2) * 2 * COLUMN].rearrange(
-                            "p (jl n u) -> p jl n u", jl=2, u=2
-                        ),
-                        in_=by_pass[:, g],
-                    )
+                odd = (j0 // 2) % 2
+                x_t = psum.tile([P, 2, 2 * P], F32, tag=("v" if odd else "kq"))
+                for u in range(2):
+                    for jl in range(2):
+                        nc.tensor.transpose(x_t[:, u, jl * P : (jl + 1) * P], sorted_words[:, j0 + jl, u, :], ident[:])
+                copy = nc.vector.tensor_copy if odd else nc.scalar.copy
+                copy(
+                    out=grouped_words[:, :, j0 * 2 * COLUMN : (j0 + 2) * 2 * COLUMN].rearrange("p g (m u) -> p g m u", u=2),
+                    in_=x_t[:].rearrange("p u (m g) -> p g m u", g=PASSES),
+                )
             for g in range(PASSES):
                 nc.vector.quantize_mx(
                     out=x_codes[:, g, half * BANK : (half + 1) * BANK].bitcast(FP8X4),
@@ -145,101 +144,142 @@ def tile_attentionconv_kernel(tc, x, W_qkv_words, W_qkv_scales, b_qkv, out):
                     in_=grouped[:, g, 4 * half * BANK : 4 * (half + 1) * BANK],
                 )
 
-        def project(n_tile, half):
-            acc = psum.tile([P, BANK], F32, tag="acc")
-            features = slice(n_tile * P, (n_tile + 1) * P)
-            patches = slice(half * BANK, (half + 1) * BANK)
-            for g in range(PASSES):
-                nc.tensor.matmul_mx(
-                    out=acc[:],
-                    lhsT=w_words[:, g, features].bitcast(FP8X4),
-                    lhsT_scale=w_scales[:, g, features],
-                    rhs=x_codes[:, g, patches].bitcast(FP8X4),
-                    rhs_scale=x_scales[:, g, patches],
-                    start=(g == 0),
-                    stop=(g == PASSES - 1),
-                )
-            return acc
+        def project(tag, section, channel):
+            banks = {}
+            for half in range(HALVES):
+                for upper in range(2):
+                    acc = psum.tile([P, BANK], F32, tag=tag)
+                    first = section * D + (2 * channel + upper) * P
+                    for g in range(PASSES):
+                        nc.tensor.matmul_mx(
+                            out=acc[:],
+                            lhsT=w_words[:, g, first : first + P].bitcast(FP8X4),
+                            lhsT_scale=w_scales[:, g, first : first + P],
+                            rhs=x_codes[:, g, half * BANK : (half + 1) * BANK].bitcast(FP8X4),
+                            rhs_scale=x_scales[:, g, half * BANK : (half + 1) * BANK],
+                            start=(g == 0),
+                            stop=(g == PASSES - 1),
+                        )
+                    banks[(upper, half)] = acc
+            return banks
+
+        def bias_of(section, channel, upper):
+            column = section * E_TILES + 2 * channel + upper
+            return bias[:, column : column + 1]
+
+        def project_k(channel):
+            k_ps = project("kq", 1, channel)
+            k_sb = work.tile([P, 2, PATCHES], F32)
+            for half in range(HALVES):
+                for upper in range(2):
+                    nc.scalar.activation(
+                        out=k_sb[:, upper, half * BANK : (half + 1) * BANK],
+                        in_=k_ps[(upper, half)][:],
+                        func=ACT.Identity,
+                        bias=bias_of(1, channel, upper),
+                        scale=1.0,
+                    )
+            return k_sb
 
         out_rows = out.rearrange("b c (m r) w -> c m b (r w)", r=PATCH // 2)
-        for channel in range(CHANNELS):
-            result = work.tile([P, GRID, GRID, 2, BATCH], F32)
-            for upper in range(2):
-                et = 2 * channel + upper
-                b_q = bias[:, et : et + 1]
-                b_k = bias[:, E_TILES + et : E_TILES + et + 1]
-                b_v = bias[:, 2 * E_TILES + et : 2 * E_TILES + et + 1]
 
-                k_sb = work.tile([P, PATCHES], F32)
-                kv_pad = work.tile([P, GRID, PAD + COLUMN + PAD], F32)
-                nc.scalar.copy(
-                    out=kv_pad[:].rearrange("p j (k w) -> p j k w", w=PAD)[:, :, 0 : COLUMN // PAD + 2 : COLUMN // PAD + 1, :],
-                    in_=edge[:, et : et + 1].unsqueeze(2).unsqueeze(3).to_broadcast([P, GRID, 2, PAD]),
-                )
-                for half in range(HALVES):
-                    k_ps = project(E_TILES + et, half)
-                    nc.scalar.activation(out=k_sb[:, half * BANK : (half + 1) * BANK], in_=k_ps[:], func=ACT.Identity, bias=b_k, scale=1.0)
-                for half in range(HALVES):
-                    v_ps = project(2 * E_TILES + et, half)
-                    nc.vector.scalar_tensor_tensor(
-                        out=kv_pad[:, half * J_BANK : (half + 1) * J_BANK, PAD : PAD + COLUMN],
-                        in0=v_ps[:].rearrange("p (j n) -> p j n", n=COLUMN),
-                        scalar=b_v,
-                        in1=k_sb[:, half * BANK : (half + 1) * BANK].rearrange("p (j n) -> p j n", n=COLUMN),
-                        op0=ALU.add,
-                        op1=ALU.mult,
-                    )
-
-                rows_pad = work.tile([P, GRID + 2, COLUMN], F32)
-                nc.scalar.copy(
-                    out=rows_pad[:, 0 : GRID + 2 : GRID + 1, :],
-                    in_=edge_rows[:, et : et + 1].unsqueeze(2).to_broadcast([P, 2, COLUMN]),
-                )
-                inner = rows_pad[:, 1 : GRID + 1, :]
-                nc.vector.scalar_tensor_tensor(
-                    out=inner,
-                    in0=kv_pad[:, :, PAD - BATCH : PAD - BATCH + COLUMN],
-                    scalar=taps[:, 2 + upper : 3 + upper],
-                    in1=kv_pad[:, :, PAD : PAD + COLUMN],
-                    op0=ALU.mult,
-                    op1=ALU.add,
-                )
-                nc.vector.scalar_tensor_tensor(
-                    out=inner,
-                    in0=kv_pad[:, :, PAD + BATCH : PAD + BATCH + COLUMN],
-                    scalar=taps[:, 4 + upper : 5 + upper],
-                    in1=inner,
-                    op0=ALU.mult,
-                    op1=ALU.add,
-                )
-
-                window = work.tile([P, GRID, COLUMN], F32)
-                nc.vector.scalar_tensor_tensor(
-                    out=window[:], in0=rows_pad[:, 0:GRID, :], scalar=taps[:, 0:1], in1=inner, op0=ALU.mult, op1=ALU.add
-                )
-                nc.vector.scalar_tensor_tensor(
-                    out=window[:], in0=rows_pad[:, 2 : GRID + 2, :], scalar=taps[:, 1:2], in1=window[:], op0=ALU.mult, op1=ALU.add
-                )
-
-                for half in range(HALVES):
-                    q_ps = project(et, half)
-                    js = slice(half * J_BANK, (half + 1) * J_BANK)
-                    nc.vector.scalar_tensor_tensor(
-                        out=result[:, js, :, upper, :],
-                        in0=q_ps[:].rearrange("p (j i b) -> p j i b", i=GRID, b=BATCH),
-                        scalar=b_q,
-                        in1=window[:, js, :].rearrange("p j (i b) -> p j i b", b=BATCH),
-                        op0=ALU.add,
-                        op1=ALU.mult,
-                    )
-
+        def store(channel, result, copies):
             image_rows = work.tile([P, PATCH // 2, GRID, PATCH], F32)
             for j0 in range(0, GRID, 4):
-                out_t = psum_t.tile([P, 4, P], F32, tag="tr")
+                out_t = psum.tile([P, 4, P], F32, tag="kq")
                 for jl in range(4):
                     nc.tensor.transpose(out_t[:, jl, :], result[:, j0 + jl].rearrange("p i h b -> p (i h b)"), ident[:])
-                nc.scalar.copy(
+                copies[(j0 // 4) % len(copies)](
                     out=image_rows[:, :, j0 : j0 + 4, :],
                     in_=out_t[:].rearrange("p j (r s) -> p r j s", s=PATCH),
                 )
             nc.sync.dma_start(out=out_rows[channel], in_=image_rows[:].rearrange("p r j s -> p (r j s)"))
+
+        k_sb = project_k(0)
+        v_ps = project("v", 2, 0)
+        result = None
+        for channel in range(CHANNELS):
+            kv_pad = work.tile([P, 2, GRID, PAD + COLUMN + PAD], F32)
+            rows_pad = work.tile([P, 2, GRID + 2, COLUMN], F32)
+            for upper in range(2):
+                et = 2 * channel + upper
+                nc.scalar.copy(
+                    out=kv_pad[:, upper].rearrange("p j (k w) -> p j k w", w=PAD)[:, :, 0 : COLUMN // PAD + 2 : COLUMN // PAD + 1, :],
+                    in_=edge[:, et : et + 1].unsqueeze(2).unsqueeze(3).to_broadcast([P, GRID, 2, PAD]),
+                )
+                nc.scalar.copy(
+                    out=rows_pad[:, upper, 0 : GRID + 2 : GRID + 1, :],
+                    in_=edge_rows[:, et : et + 1].unsqueeze(2).to_broadcast([P, 2, COLUMN]),
+                )
+            for half in range(HALVES):
+                for upper in range(2):
+                    nc.vector.scalar_tensor_tensor(
+                        out=kv_pad[:, upper, half * J_BANK : (half + 1) * J_BANK, PAD : PAD + COLUMN],
+                        in0=v_ps[(upper, half)][:].rearrange("p (j n) -> p j n", n=COLUMN),
+                        scalar=bias_of(2, channel, upper),
+                        in1=k_sb[:, upper, half * BANK : (half + 1) * BANK].rearrange("p (j n) -> p j n", n=COLUMN),
+                        op0=ALU.add,
+                        op1=ALU.mult,
+                    )
+
+            if channel > 0:
+                store(channel - 1, result, (nc.scalar.copy,))
+            if channel + 1 < CHANNELS:
+                k_sb = project_k(channel + 1)
+            q_ps = project("kq", 0, channel)
+            if channel + 1 < CHANNELS:
+                v_ps = project("v", 2, channel + 1)
+
+            for upper in range(2):
+                nc.vector.scalar_tensor_tensor(
+                    out=rows_pad[:, upper, 1 : GRID + 1, :],
+                    in0=kv_pad[:, upper, :, PAD - BATCH : PAD - BATCH + COLUMN],
+                    scalar=taps[:, 2 + upper : 3 + upper],
+                    in1=kv_pad[:, upper, :, PAD : PAD + COLUMN],
+                    op0=ALU.mult,
+                    op1=ALU.add,
+                )
+            for upper in range(2):
+                nc.vector.scalar_tensor_tensor(
+                    out=rows_pad[:, upper, 1 : GRID + 1, :],
+                    in0=kv_pad[:, upper, :, PAD + BATCH : PAD + BATCH + COLUMN],
+                    scalar=taps[:, 4 + upper : 5 + upper],
+                    in1=rows_pad[:, upper, 1 : GRID + 1, :],
+                    op0=ALU.mult,
+                    op1=ALU.add,
+                )
+
+            window = work.tile([P, 2, GRID, COLUMN], F32)
+            for upper in range(2):
+                nc.vector.scalar_tensor_tensor(
+                    out=window[:, upper],
+                    in0=rows_pad[:, upper, 0:GRID, :],
+                    scalar=taps[:, 0:1],
+                    in1=rows_pad[:, upper, 1 : GRID + 1, :],
+                    op0=ALU.mult,
+                    op1=ALU.add,
+                )
+            for upper in range(2):
+                nc.vector.scalar_tensor_tensor(
+                    out=window[:, upper],
+                    in0=rows_pad[:, upper, 2 : GRID + 2, :],
+                    scalar=taps[:, 1:2],
+                    in1=window[:, upper],
+                    op0=ALU.mult,
+                    op1=ALU.add,
+                )
+
+            result = work.tile([P, GRID, GRID, 2, BATCH], F32)
+            for half in range(HALVES):
+                js = slice(half * J_BANK, (half + 1) * J_BANK)
+                for upper in range(2):
+                    nc.vector.scalar_tensor_tensor(
+                        out=result[:, js, :, upper, :],
+                        in0=q_ps[(upper, half)][:].rearrange("p (j i b) -> p j i b", i=GRID, b=BATCH),
+                        scalar=bias_of(0, channel, upper),
+                        in1=window[:, upper, js, :].rearrange("p j (i b) -> p j i b", b=BATCH),
+                        op0=ALU.add,
+                        op1=ALU.mult,
+                    )
+
+        store(CHANNELS - 1, result, (nc.scalar.copy, nc.vector.tensor_copy))

@@ -227,6 +227,15 @@ def tile_attentionconv_kernel(tc, x, W_qkv_words, W_qkv_scales, b_qkv, out):
             if channel + 1 < CHANNELS:
                 k_sb = project_k(channel + 1)
             q_ps = project("kq", 0, channel)
+            q_sb = work.tile([P, 2, BANK], F32)
+            for upper in range(2):
+                nc.scalar.activation(
+                    out=q_sb[:, upper, :],
+                    in_=q_ps[(upper, 1)][:],
+                    func=ACT.Identity,
+                    bias=bias_of(0, channel, upper),
+                    scale=1.0,
+                )
             if channel + 1 < CHANNELS:
                 v_ps = project("v", 2, channel + 1)
 
@@ -270,16 +279,21 @@ def tile_attentionconv_kernel(tc, x, W_qkv_words, W_qkv_scales, b_qkv, out):
                 )
 
             result = work.tile([P, GRID, GRID, 2, BATCH], F32)
-            for half in range(HALVES):
-                js = slice(half * J_BANK, (half + 1) * J_BANK)
-                for upper in range(2):
-                    nc.vector.scalar_tensor_tensor(
-                        out=result[:, js, :, upper, :],
-                        in0=q_ps[(upper, half)][:].rearrange("p (j i b) -> p j i b", i=GRID, b=BATCH),
-                        scalar=bias_of(0, channel, upper),
-                        in1=window[:, upper, js, :].rearrange("p j (i b) -> p j i b", b=BATCH),
-                        op0=ALU.add,
-                        op1=ALU.mult,
-                    )
+            for upper in range(2):
+                nc.vector.scalar_tensor_tensor(
+                    out=result[:, 0:J_BANK, :, upper, :],
+                    in0=q_ps[(upper, 0)][:].rearrange("p (j i b) -> p j i b", i=GRID, b=BATCH),
+                    scalar=bias_of(0, channel, upper),
+                    in1=window[:, upper, 0:J_BANK, :].rearrange("p j (i b) -> p j i b", b=BATCH),
+                    op0=ALU.add,
+                    op1=ALU.mult,
+                )
+            for upper in range(2):
+                nc.gpsimd.tensor_tensor(
+                    out=result[:, J_BANK:GRID, :, upper, :],
+                    in0=q_sb[:, upper, :].rearrange("p (j i b) -> p j i b", i=GRID, b=BATCH),
+                    in1=window[:, upper, J_BANK:GRID, :].rearrange("p j (i b) -> p j i b", b=BATCH),
+                    op=ALU.mult,
+                )
 
         store(CHANNELS - 1, result, (nc.scalar.copy, nc.vector.tensor_copy))

@@ -27,6 +27,7 @@ HALVES = PATCHES // BANK
 COLUMN = GRID * BATCH
 J_BANK = BANK // COLUMN
 E_TILES = D // P
+QUARTERS = 4
 PAD = 8
 
 FLOPS = 2 * PATCHES * D * 3 * D
@@ -40,10 +41,10 @@ def tile_attentionconv_kernel(tc, x, W_qkv_words, W_qkv_scales, b_qkv, out):
         work = ctx.enter_context(tc.tile_pool(name="work", bufs=2))
         psum = ctx.enter_context(tc.psum_pool(name="psum", bufs=4))
 
-        x_rows = x.rearrange("b (g c) (i r) w -> c i (b g) (r w)", g=2, c=2, i=GRID, r=PATCH)
-        x_sb = keep.tile([P, 2, PATCH * WIDTH], BF16)
-        for c in range(2):
-            nc.sync.dma_start(out=x_sb[:, c, :], in_=x_rows[c])
+        x_rows = x.rearrange("b (g c) (i q r) w -> c q i (b g) (r w)", g=2, c=2, i=GRID, q=2)
+        x_sb = keep.tile([P, QUARTERS, PATCH // 2 * WIDTH], BF16)
+        for quarter in range(QUARTERS):
+            nc.sync.dma_start(out=x_sb[:, quarter, :], in_=x_rows[quarter // 2, quarter % 2])
 
         bias_rows = keep.tile([P, P], BF16)
         nc.vector.memset(bias_rows[:], 0.0)
@@ -52,20 +53,17 @@ def tile_attentionconv_kernel(tc, x, W_qkv_words, W_qkv_scales, b_qkv, out):
         w_scales = keep.tile([P, PASSES, 3 * D], U8, align_bytes=64)
         nc.vector.memset(w_scales[:].rearrange("p g n -> p (g n)").bitcast(I32), 0)
         for quad in range(4):
-            nc.sync.dma_start(
-                out=w_scales[32 * quad : 32 * quad + 4, :, :].bitcast(I32),
-                in_=W_qkv_scales[:, 4 * quad : 4 * quad + 4, :].rearrange("g r n -> r g n").bitcast(I32),
+            nc.scalar.dma_start(
+                out=w_scales[32 * quad : 32 * quad + 4, :, :].bitcast(F32),
+                in_=W_qkv_scales[:, 4 * quad : 4 * quad + 4, :].rearrange("g r n -> r g n").bitcast(F32),
             )
 
         w_words = keep.tile([P, PASSES, 3 * D], U32, align_bytes=64)
         for section in (1, 2, 0):
-            for g in range(PASSES):
-                nc.sync.dma_start(
-                    out=w_words[:, g, section * D : (section + 1) * D].bitcast(I32),
-                    in_=W_qkv_words[g]
-                    .rearrange("p n t -> p (n t)")[:, 4 * section * D : 4 * (section + 1) * D]
-                    .bitcast(I32),
-                )
+            nc.sync.dma_start(
+                out=w_words[:, :, section * D : (section + 1) * D].bitcast(I32),
+                in_=W_qkv_words.rearrange("g p n t -> p g (n t)")[:, :, 4 * section * D : 4 * (section + 1) * D].bitcast(I32),
+            )
 
         ident = keep.tile([P, P], F32)
         make_identity(nc, ident[:])
@@ -107,18 +105,15 @@ def tile_attentionconv_kernel(tc, x, W_qkv_words, W_qkv_scales, b_qkv, out):
             op=ALU.mult,
         )
 
-        x_words = (
-            x_sb[:]
-            .rearrange("p c e -> p (c e)")
-            .bitcast(F32)
-            .rearrange("p (cr j s u) -> p u j cr s", cr=2 * PATCH, j=GRID, s=4, u=2)
-        )
+        x_words = x_sb[:].bitcast(F32).rearrange("p q (r j s u) -> p q u j r s", j=GRID, s=4, u=2)
         sorted_words = keep.tile([P, GRID, 2, P], F32)
-        for j0 in range(0, GRID, 4):
+        for quarter in range(QUARTERS):
             for u in range(2):
                 nc.vector.tensor_copy(
-                    out=sorted_words[:, j0 : j0 + 4, u, :].rearrange("p j (cr s) -> p j cr s", s=4),
-                    in_=x_words[:, u, j0 : j0 + 4],
+                    out=sorted_words[:, :, u, quarter * P // QUARTERS : (quarter + 1) * P // QUARTERS].rearrange(
+                        "p j (r s) -> p j r s", s=4
+                    ),
+                    in_=x_words[:, quarter, u],
                 )
 
         grouped = keep.tile([P, PASSES, 4 * PATCHES], BF16, align_bytes=64)
@@ -144,42 +139,37 @@ def tile_attentionconv_kernel(tc, x, W_qkv_words, W_qkv_scales, b_qkv, out):
                     in_=grouped[:, g, 4 * half * BANK : 4 * (half + 1) * BANK],
                 )
 
-        def project(tag, section, channel):
-            banks = {}
-            for half in range(HALVES):
-                for upper in range(2):
-                    acc = psum.tile([P, BANK], F32, tag=tag)
-                    first = section * D + (2 * channel + upper) * P
-                    for g in range(PASSES):
-                        nc.tensor.matmul_mx(
-                            out=acc[:],
-                            lhsT=w_words[:, g, first : first + P].bitcast(FP8X4),
-                            lhsT_scale=w_scales[:, g, first : first + P],
-                            rhs=x_codes[:, g, half * BANK : (half + 1) * BANK].bitcast(FP8X4),
-                            rhs_scale=x_scales[:, g, half * BANK : (half + 1) * BANK],
-                            start=(g == 0),
-                            stop=(g == PASSES - 1),
-                        )
-                    banks[(upper, half)] = acc
-            return banks
+        def project(tag, section, channel, half, banks):
+            for upper in range(2):
+                acc = psum.tile([P, BANK], F32, tag=tag)
+                first = section * D + (2 * channel + upper) * P
+                for g in range(PASSES):
+                    nc.tensor.matmul_mx(
+                        out=acc[:],
+                        lhsT=w_words[:, g, first : first + P].bitcast(FP8X4),
+                        lhsT_scale=w_scales[:, g, first : first + P],
+                        rhs=x_codes[:, g, half * BANK : (half + 1) * BANK].bitcast(FP8X4),
+                        rhs_scale=x_scales[:, g, half * BANK : (half + 1) * BANK],
+                        start=(g == 0),
+                        stop=(g == PASSES - 1),
+                    )
+                banks[(upper, half)] = acc
 
         def bias_of(section, channel, upper):
             column = section * E_TILES + 2 * channel + upper
             return bias[:, column : column + 1]
 
-        def project_k(channel):
-            k_ps = project("kq", 1, channel)
-            k_sb = work.tile([P, 2, PATCHES], F32)
-            for half in range(HALVES):
-                for upper in range(2):
-                    nc.scalar.activation(
-                        out=k_sb[:, upper, half * BANK : (half + 1) * BANK],
-                        in_=k_ps[(upper, half)][:],
-                        func=ACT.Identity,
-                        bias=bias_of(1, channel, upper),
-                        scale=1.0,
-                    )
-            return k_sb
+        def project_k(channel, half, k_sb):
+            k_ps = {}
+            project("kq", 1, channel, half, k_ps)
+            for upper in range(2):
+                nc.scalar.activation(
+                    out=k_sb[:, upper, half * BANK : (half + 1) * BANK],
+                    in_=k_ps[(upper, half)][:],
+                    func=ACT.Identity,
+                    bias=bias_of(1, channel, upper),
+                    scale=1.0,
+                )
 
         out_rows = out.rearrange("b c (m r) w -> c m b (r w)", r=PATCH // 2)
 
@@ -195,8 +185,11 @@ def tile_attentionconv_kernel(tc, x, W_qkv_words, W_qkv_scales, b_qkv, out):
                 )
             nc.sync.dma_start(out=out_rows[channel], in_=image_rows[:].rearrange("p r j s -> p (r j s)"))
 
-        k_sb = project_k(0)
-        v_ps = project("v", 2, 0)
+        k_sb = work.tile([P, 2, PATCHES], F32, tag="k_sb")
+        v_ps = {}
+        for half in range(HALVES):
+            project_k(0, half, k_sb)
+            project("v", 2, 0, half, v_ps)
         result = None
         for channel in range(CHANNELS):
             kv_pad = work.tile([P, 2, GRID, PAD + COLUMN + PAD], F32)
@@ -225,8 +218,12 @@ def tile_attentionconv_kernel(tc, x, W_qkv_words, W_qkv_scales, b_qkv, out):
             if channel > 0:
                 store(channel - 1, result, (nc.scalar.copy,))
             if channel + 1 < CHANNELS:
-                k_sb = project_k(channel + 1)
-            q_ps = project("kq", 0, channel)
+                k_sb = work.tile([P, 2, PATCHES], F32, tag="k_sb")
+                for half in range(HALVES):
+                    project_k(channel + 1, half, k_sb)
+            q_ps = {}
+            for half in range(HALVES):
+                project("kq", 0, channel, half, q_ps)
             q_sb = work.tile([P, 2, BANK], F32)
             for upper in range(2):
                 nc.scalar.activation(
@@ -237,7 +234,9 @@ def tile_attentionconv_kernel(tc, x, W_qkv_words, W_qkv_scales, b_qkv, out):
                     scale=1.0,
                 )
             if channel + 1 < CHANNELS:
-                v_ps = project("v", 2, channel + 1)
+                v_ps = {}
+                for half in range(HALVES):
+                    project("v", 2, channel + 1, half, v_ps)
 
             for upper in range(2):
                 nc.vector.scalar_tensor_tensor(

@@ -65,11 +65,10 @@ def tile_attentionconv_kernel(tc, x, W_qkv_words, W_qkv_scales, b_qkv, out):
                 in_=W_qkv_words.rearrange("g p n t -> p g (n t)")[:, :, 4 * section * D : 4 * (section + 1) * D].bitcast(I32),
             )
 
-        ident = keep.tile([P, P], F32)
-        make_identity(nc, ident[:])
-
         p_index = keep.tile([P, 1], I32)
         nc.gpsimd.iota(p_index[:], pattern=[[0, 1]], base=0, channel_multiplier=1)
+        ident = keep.tile([P, P], F32)
+        make_identity(nc, ident[:])
         rs_int = keep.tile([P, 2], I32)
         nc.vector.tensor_single_scalar(out=rs_int[:, 0:1], in_=p_index[:], scalar=PATCH - 1, op=ALU.bitwise_and)
         nc.vector.tensor_single_scalar(out=rs_int[:, 1:2], in_=p_index[:], scalar=4, op=ALU.logical_shift_right)
@@ -87,18 +86,19 @@ def tile_attentionconv_kernel(tc, x, W_qkv_words, W_qkv_scales, b_qkv, out):
         nc.scalar.activation(out=taps[:], in_=exponents[:], func=ACT.Exp)
 
         bias_rows_f32 = keep.tile([P, P], F32)
-        nc.vector.tensor_copy(out=bias_rows_f32[:], in_=bias_rows[:])
+        nc.scalar.copy(out=bias_rows_f32[:], in_=bias_rows[:])
         bias_t = psum.tile([P, BANK], F32, tag="kq")
         nc.tensor.transpose(bias_t[:, 0:P], bias_rows_f32[:], ident[:])
         bias = keep.tile([P, 3 * E_TILES], F32)
-        nc.vector.tensor_copy(out=bias[:], in_=bias_t[:, 0 : 3 * E_TILES])
+        nc.scalar.copy(out=bias[:], in_=bias_t[:, 0 : 3 * E_TILES])
 
         edge = keep.tile([P, E_TILES], F32)
-        nc.vector.tensor_tensor(out=edge[:], in0=bias[:, E_TILES : 2 * E_TILES], in1=bias[:, 2 * E_TILES : 3 * E_TILES], op=ALU.mult)
+        nc.gpsimd.tensor_tensor(out=edge[:], in0=bias[:, E_TILES : 2 * E_TILES], in1=bias[:, 2 * E_TILES : 3 * E_TILES], op=ALU.mult)
         tap_sum = keep.tile([P, 2], F32)
-        nc.vector.scalar_tensor_tensor(out=tap_sum[:], in0=taps[:, 2:4], scalar=1.0, in1=taps[:, 4:6], op0=ALU.add, op1=ALU.add)
+        nc.gpsimd.tensor_tensor(out=tap_sum[:], in0=taps[:, 2:4], in1=taps[:, 4:6], op=ALU.add)
+        nc.gpsimd.tensor_scalar_add(out=tap_sum[:], in0=tap_sum[:], scalar1=1.0)
         edge_rows = keep.tile([P, E_TILES], F32)
-        nc.vector.tensor_tensor(
+        nc.gpsimd.tensor_tensor(
             out=edge_rows[:].rearrange("p (c h) -> p c h", h=2),
             in0=edge[:].rearrange("p (c h) -> p c h", h=2),
             in1=tap_sum[:].unsqueeze(1).to_broadcast([P, CHANNELS, 2]),

@@ -87,7 +87,7 @@ def tile_attentionconv_kernel(tc, x, W_qkv_words, W_qkv_scales, b_qkv, out):
 
         bias_rows_f32 = keep.tile([P, P], F32)
         nc.scalar.copy(out=bias_rows_f32[:], in_=bias_rows[:])
-        bias_t = psum.tile([P, BANK], F32, tag="kq")
+        bias_t = psum.tile([P, BANK], F32, tag="kq", bufs=4)
         nc.tensor.transpose(bias_t[:, 0:P], bias_rows_f32[:], ident[:])
         bias = keep.tile([P, 3 * E_TILES], F32)
         nc.scalar.copy(out=bias[:], in_=bias_t[:, 0 : 3 * E_TILES])
@@ -123,7 +123,10 @@ def tile_attentionconv_kernel(tc, x, W_qkv_words, W_qkv_scales, b_qkv, out):
         for half in range(HALVES):
             for j0 in range(half * J_BANK, (half + 1) * J_BANK, 2):
                 odd = (j0 // 2) % 2
-                x_t = psum.tile([P, 2, 2 * P], F32, tag=("v" if odd else "kq"))
+                if odd:
+                    x_t = psum.tile([P, 2, 2 * P], F32, tag=("v" if (j0 // 4) % 2 == 0 else "sum"), bufs=2)
+                else:
+                    x_t = psum.tile([P, 2, 2 * P], F32, tag="kq", bufs=4)
                 for u in range(2):
                     for jl in range(2):
                         nc.tensor.transpose(x_t[:, u, jl * P : (jl + 1) * P], sorted_words[:, j0 + jl, u, :], ident[:])
@@ -139,9 +142,10 @@ def tile_attentionconv_kernel(tc, x, W_qkv_words, W_qkv_scales, b_qkv, out):
                     in_=grouped[:, g, 4 * half * BANK : 4 * (half + 1) * BANK],
                 )
 
-        def project(tag, section, channel, half, banks):
+        def project(tag, bufs, section, channel, half):
+            banks = []
             for upper in range(2):
-                acc = psum.tile([P, BANK], F32, tag=tag)
+                acc = psum.tile([P, BANK], F32, tag=tag, bufs=bufs)
                 first = section * D + (2 * channel + upper) * P
                 for g in range(PASSES):
                     nc.tensor.matmul_mx(
@@ -153,47 +157,37 @@ def tile_attentionconv_kernel(tc, x, W_qkv_words, W_qkv_scales, b_qkv, out):
                         start=(g == 0),
                         stop=(g == PASSES - 1),
                     )
-                banks[(upper, half)] = acc
+                banks.append(acc)
+            return banks
 
         def bias_of(section, channel, upper):
             column = section * E_TILES + 2 * channel + upper
             return bias[:, column : column + 1]
 
         def project_k(channel, half, k_sb):
-            k_ps = {}
-            project("kq", 1, channel, half, k_ps)
+            k_ps = project("kq", 4, 1, channel, half)
             for upper in range(2):
                 nc.scalar.activation(
                     out=k_sb[:, upper, half * BANK : (half + 1) * BANK],
-                    in_=k_ps[(upper, half)][:],
+                    in_=k_ps[upper][:],
                     func=ACT.Identity,
                     bias=bias_of(1, channel, upper),
                     scale=1.0,
                 )
 
-        out_rows = out.rearrange("b c (m r) w -> c m b (r w)", r=PATCH // 2)
+        def project_q(channel, q_sb):
+            for half in range(HALVES):
+                q_ps = project("kq", 4, 0, channel, half)
+                for upper in range(2):
+                    nc.scalar.activation(
+                        out=q_sb[:, half * J_BANK : (half + 1) * J_BANK, :, upper, :],
+                        in_=q_ps[upper][:].rearrange("p (j i b) -> p j i b", i=GRID, b=BATCH),
+                        func=ACT.Identity,
+                        bias=bias_of(0, channel, upper),
+                        scale=1.0,
+                    )
 
-        def store(channel, result, copies):
-            image_rows = work.tile([P, PATCH // 2, GRID, PATCH], F32)
-            for j0 in range(0, GRID, 4):
-                out_t = psum.tile([P, 4, P], F32, tag="kq")
-                for jl in range(4):
-                    nc.tensor.transpose(out_t[:, jl, :], result[:, j0 + jl].rearrange("p i h b -> p (i h b)"), ident[:])
-                copies[(j0 // 4) % len(copies)](
-                    out=image_rows[:, :, j0 : j0 + 4, :],
-                    in_=out_t[:].rearrange("p j (r s) -> p r j s", s=PATCH),
-                )
-            nc.sync.dma_start(out=out_rows[channel], in_=image_rows[:].rearrange("p r j s -> p (r j s)"))
-
-        k_sb = work.tile([P, 2, PATCHES], F32, tag="k_sb")
-        v_ps = {}
-        for half in range(HALVES):
-            project_k(0, half, k_sb)
-            project("v", 2, 0, half, v_ps)
-        result = None
-        for channel in range(CHANNELS):
-            kv_pad = work.tile([P, 2, GRID, PAD + COLUMN + PAD], F32)
-            rows_pad = work.tile([P, 2, GRID + 2, COLUMN], F32)
+        def borders(channel, kv_pad, rows_pad):
             for upper in range(2):
                 et = 2 * channel + upper
                 nc.scalar.copy(
@@ -201,98 +195,192 @@ def tile_attentionconv_kernel(tc, x, W_qkv_words, W_qkv_scales, b_qkv, out):
                     in_=edge[:, et : et + 1].unsqueeze(2).unsqueeze(3).to_broadcast([P, GRID, 2, PAD]),
                 )
                 nc.scalar.copy(
-                    out=rows_pad[:, upper, 0 : GRID + 2 : GRID + 1, :],
-                    in_=edge_rows[:, et : et + 1].unsqueeze(2).to_broadcast([P, 2, COLUMN]),
+                    out=rows_pad[:, 0 : GRID + 2 : GRID + 1, :, upper, :],
+                    in_=edge_rows[:, et : et + 1].unsqueeze(2).unsqueeze(3).to_broadcast([P, 2, GRID, BATCH]),
                 )
-            for half in range(HALVES):
-                for upper in range(2):
-                    nc.vector.scalar_tensor_tensor(
-                        out=kv_pad[:, upper, half * J_BANK : (half + 1) * J_BANK, PAD : PAD + COLUMN],
-                        in0=v_ps[(upper, half)][:].rearrange("p (j n) -> p j n", n=COLUMN),
-                        scalar=bias_of(2, channel, upper),
-                        in1=k_sb[:, upper, half * BANK : (half + 1) * BANK].rearrange("p (j n) -> p j n", n=COLUMN),
-                        op0=ALU.add,
-                        op1=ALU.mult,
-                    )
 
-            if channel > 0:
-                store(channel - 1, result, (nc.scalar.copy,))
-            if channel + 1 < CHANNELS:
-                k_sb = work.tile([P, 2, PATCHES], F32, tag="k_sb")
-                for half in range(HALVES):
-                    project_k(channel + 1, half, k_sb)
-            q_ps = {}
-            for half in range(HALVES):
-                project("kq", 0, channel, half, q_ps)
-            q_sb = work.tile([P, 2, BANK], F32)
-            for upper in range(2):
-                nc.scalar.activation(
-                    out=q_sb[:, upper, :],
-                    in_=q_ps[(upper, 1)][:],
-                    func=ACT.Identity,
-                    bias=bias_of(0, channel, upper),
-                    scale=1.0,
+        def multiply_kv(channel, half, upper, v_ps, k_sb, kv_pad):
+            nc.vector.scalar_tensor_tensor(
+                out=kv_pad[:, upper, half * J_BANK : (half + 1) * J_BANK, PAD : PAD + COLUMN],
+                in0=v_ps[upper][:].rearrange("p (j n) -> p j n", n=COLUMN),
+                scalar=bias_of(2, channel, upper),
+                in1=k_sb[:, upper, half * BANK : (half + 1) * BANK].rearrange("p (j n) -> p j n", n=COLUMN),
+                op0=ALU.add,
+                op1=ALU.mult,
+            )
+
+        def flat(columns):
+            return columns.rearrange("p j i h b -> p (j i h b)")
+
+        out_rows = out.rearrange("b c (m r) w -> c m b (r w)", r=PATCH // 2)
+
+        def store_right(channel, result, image_rows, copies):
+            for j0 in range(0, J_BANK, 4):
+                out_t = psum.tile([P, 4, P], F32, tag="kq", bufs=4)
+                for jl in range(4):
+                    nc.tensor.transpose(out_t[:, jl, :], result[:, j0 + jl, :], ident[:])
+                copies[(j0 // 4) % len(copies)](
+                    out=image_rows[:, :, J_BANK + j0 : J_BANK + j0 + 4, :],
+                    in_=out_t[:].rearrange("p j (r s) -> p r j s", s=PATCH),
                 )
-            if channel + 1 < CHANNELS:
-                v_ps = {}
-                for half in range(HALVES):
-                    project("v", 2, channel + 1, half, v_ps)
+            nc.sync.dma_start(out=out_rows[channel], in_=image_rows[:].rearrange("p r j s -> p (r j s)"))
+
+        k_sbs = {}
+        v_left = {}
+        kv_pads = {}
+        rows_pads = {}
+        q_sbs = {}
+        k_sb = work.tile([P, 2, PATCHES], F32, tag="k_sb")
+        kv_pad = work.tile([P, 2, GRID, PAD + COLUMN + PAD], F32, tag="kv_pad")
+        rows_pad = work.tile([P, GRID + 2, GRID, 2, BATCH], F32, tag="rows_pad")
+        project_k(0, 0, k_sb)
+        v_ps0 = project("v", 2, 2, 0, 0)
+        project_k(0, 1, k_sb)
+        v_ps1 = project("sum", 2, 2, 0, 1)
+        borders(0, kv_pad, rows_pad)
+        for upper in range(2):
+            multiply_kv(0, 0, upper, v_ps0, k_sb, kv_pad)
+        for upper in range(2):
+            multiply_kv(0, 1, upper, v_ps1, k_sb, kv_pad)
+        kv_pads[0] = kv_pad
+        rows_pads[0] = rows_pad
+        q_sb = work.tile([P, GRID, GRID, 2, BATCH], F32, tag="q_sb")
+        project_q(0, q_sb)
+        q_sbs[0] = q_sb
+        k_sb = work.tile([P, 2, PATCHES], F32, tag="k_sb")
+        for half in range(HALVES):
+            project_k(1, half, k_sb)
+        k_sbs[1] = k_sb
+        v_left[1] = project("v", 2, 2, 1, 0)
+
+        waiting = None
+        for channel in range(CHANNELS):
+            after = channel + 1
+            kv_pad = kv_pads[channel]
+            rows_pad = rows_pads[channel]
+            q_sb = q_sbs[channel]
 
             for upper in range(2):
                 nc.vector.scalar_tensor_tensor(
-                    out=rows_pad[:, upper, 1 : GRID + 1, :],
-                    in0=kv_pad[:, upper, :, PAD - BATCH : PAD - BATCH + COLUMN],
+                    out=rows_pad[:, 1 : GRID + 1, :, upper, :],
+                    in0=kv_pad[:, upper, :, PAD - BATCH : PAD - BATCH + COLUMN].rearrange("p j (i b) -> p j i b", b=BATCH),
                     scalar=taps[:, 2 + upper : 3 + upper],
-                    in1=kv_pad[:, upper, :, PAD : PAD + COLUMN],
+                    in1=kv_pad[:, upper, :, PAD : PAD + COLUMN].rearrange("p j (i b) -> p j i b", b=BATCH),
                     op0=ALU.mult,
                     op1=ALU.add,
                 )
             for upper in range(2):
                 nc.vector.scalar_tensor_tensor(
-                    out=rows_pad[:, upper, 1 : GRID + 1, :],
-                    in0=kv_pad[:, upper, :, PAD + BATCH : PAD + BATCH + COLUMN],
+                    out=rows_pad[:, 1 : GRID + 1, :, upper, :],
+                    in0=kv_pad[:, upper, :, PAD + BATCH : PAD + BATCH + COLUMN].rearrange("p j (i b) -> p j i b", b=BATCH),
                     scalar=taps[:, 4 + upper : 5 + upper],
-                    in1=rows_pad[:, upper, 1 : GRID + 1, :],
+                    in1=rows_pad[:, 1 : GRID + 1, :, upper, :],
                     op0=ALU.mult,
                     op1=ALU.add,
                 )
 
-            window = work.tile([P, 2, GRID, COLUMN], F32)
-            for upper in range(2):
+            from_left = work.tile([P, J_BANK, P], F32, tag="from_left")
+            nc.scalar.activation(
+                out=from_left[:].rearrange("p j n -> p (j n)"),
+                in_=flat(rows_pad[:, 0:J_BANK]),
+                func=ACT.Identity,
+                scale=taps[:, 0:1],
+            )
+            from_right = work.tile([P, J_BANK, P], F32, tag="from_right")
+            if after < CHANNELS:
+                kv_pad_after = work.tile([P, 2, GRID, PAD + COLUMN + PAD], F32, tag="kv_pad")
+                rows_pad_after = work.tile([P, GRID + 2, GRID, 2, BATCH], F32, tag="rows_pad")
+                kv_pads[after] = kv_pad_after
+                rows_pads[after] = rows_pad_after
+                multiply_kv(after, 0, 0, v_left[after], k_sbs[after], kv_pad_after)
+            nc.vector.tensor_scalar_mul(
+                out=from_right[:].rearrange("p j n -> p (j n)"),
+                in0=flat(rows_pad[:, 2 : J_BANK + 2]),
+                scalar1=taps[:, 1:2],
+            )
+            if after < CHANNELS:
+                multiply_kv(after, 0, 1, v_left[after], k_sbs[after], kv_pad_after)
+
+            if waiting is not None:
+                store_right(channel - 1, waiting[0], waiting[1], (nc.scalar.copy,))
+
+            q_t_sb = work.tile([P, J_BANK, P], F32, tag="q_t_sb")
+            for j0 in range(0, J_BANK, 4):
+                q_t = psum.tile([P, 4, P], F32, tag="kq", bufs=4)
+                for jl in range(4):
+                    nc.tensor.transpose(q_t[:, jl, :], q_sb[:, j0 + jl].rearrange("p i h b -> p (i h b)"), ident[:])
+                nc.scalar.copy(out=q_t_sb[:, j0 : j0 + 4, :], in_=q_t[:])
+
+            sums = []
+            for j0 in range(0, J_BANK, 4):
+                sum_t = psum.tile([P, 4, P], F32, tag="sum", bufs=2)
+                for jl in range(4):
+                    j = j0 + jl
+                    nc.tensor.matmul(sum_t[:, jl, :], lhsT=from_left[:, j, :], rhs=ident[:], start=True, stop=False, is_transpose=True)
+                    nc.tensor.matmul(
+                        sum_t[:, jl, :],
+                        lhsT=rows_pad[:, j + 1].rearrange("p i h b -> p (i h b)"),
+                        rhs=ident[:],
+                        start=False,
+                        stop=False,
+                        is_transpose=True,
+                    )
+                    nc.tensor.matmul(sum_t[:, jl, :], lhsT=from_right[:, j, :], rhs=ident[:], start=False, stop=True, is_transpose=True)
+                sums.append(sum_t)
+
+            if after < CHANNELS:
+                borders(after, kv_pad_after, rows_pad_after)
+
+            window = work.tile([P, J_BANK, P], F32, tag="window")
+            for j0 in range(0, J_BANK, 4):
                 nc.vector.scalar_tensor_tensor(
-                    out=window[:, upper],
-                    in0=rows_pad[:, upper, 0:GRID, :],
+                    out=window[:, j0 : j0 + 4, :].rearrange("p j n -> p (j n)"),
+                    in0=flat(rows_pad[:, J_BANK + j0 : J_BANK + j0 + 4]),
                     scalar=taps[:, 0:1],
-                    in1=rows_pad[:, upper, 1 : GRID + 1, :],
+                    in1=flat(rows_pad[:, J_BANK + j0 + 1 : J_BANK + j0 + 5]),
                     op0=ALU.mult,
                     op1=ALU.add,
                 )
-            for upper in range(2):
+            for j0 in range(0, J_BANK, 4):
                 nc.vector.scalar_tensor_tensor(
-                    out=window[:, upper],
-                    in0=rows_pad[:, upper, 2 : GRID + 2, :],
+                    out=window[:, j0 : j0 + 4, :].rearrange("p j n -> p (j n)"),
+                    in0=flat(rows_pad[:, J_BANK + j0 + 2 : J_BANK + j0 + 6]),
                     scalar=taps[:, 1:2],
-                    in1=window[:, upper],
+                    in1=window[:, j0 : j0 + 4, :].rearrange("p j n -> p (j n)"),
                     op0=ALU.mult,
                     op1=ALU.add,
                 )
-
-            result = work.tile([P, GRID, GRID, 2, BATCH], F32)
-            for upper in range(2):
-                nc.vector.scalar_tensor_tensor(
-                    out=result[:, 0:J_BANK, :, upper, :],
-                    in0=q_ps[(upper, 0)][:].rearrange("p (j i b) -> p j i b", i=GRID, b=BATCH),
-                    scalar=bias_of(0, channel, upper),
-                    in1=window[:, upper, 0:J_BANK, :].rearrange("p j (i b) -> p j i b", b=BATCH),
-                    op0=ALU.add,
-                    op1=ALU.mult,
-                )
-            for upper in range(2):
+            result = work.tile([P, J_BANK, P], F32, tag="result")
+            for j0 in (4, 0):
                 nc.gpsimd.tensor_tensor(
-                    out=result[:, J_BANK:GRID, :, upper, :],
-                    in0=q_sb[:, upper, :].rearrange("p (j i b) -> p j i b", i=GRID, b=BATCH),
-                    in1=window[:, upper, J_BANK:GRID, :].rearrange("p j (i b) -> p j i b", b=BATCH),
+                    out=result[:, j0 : j0 + 4, :].rearrange("p j n -> p (j n)"),
+                    in0=flat(q_sb[:, J_BANK + j0 : J_BANK + j0 + 4]),
+                    in1=window[:, j0 : j0 + 4, :].rearrange("p j n -> p (j n)"),
                     op=ALU.mult,
                 )
 
-        store(CHANNELS - 1, result, (nc.scalar.copy, nc.vector.tensor_copy))
+            image_rows = work.tile([P, PATCH // 2, GRID, PATCH], F32, tag="image_rows")
+            for j0 in range(0, J_BANK, 4):
+                nc.vector.tensor_tensor(
+                    out=image_rows[:, :, j0 : j0 + 4, :],
+                    in0=sums[j0 // 4][:].rearrange("p j (r s) -> p r j s", s=PATCH),
+                    in1=q_t_sb[:, j0 : j0 + 4, :].rearrange("p j (r s) -> p r j s", s=PATCH),
+                    op=ALU.mult,
+                )
+            waiting = (result, image_rows)
+
+            if after < CHANNELS:
+                v_right = project("v", 2, 2, after, 1)
+                for upper in range(2):
+                    multiply_kv(after, 1, upper, v_right, k_sbs[after], kv_pad_after)
+                q_sb_after = work.tile([P, GRID, GRID, 2, BATCH], F32, tag="q_sb")
+                project_q(after, q_sb_after)
+                q_sbs[after] = q_sb_after
+            if after + 1 < CHANNELS:
+                k_sb = work.tile([P, 2, PATCHES], F32, tag="k_sb")
+                for half in range(HALVES):
+                    project_k(after + 1, half, k_sb)
+                k_sbs[after + 1] = k_sb
+                v_left[after + 1] = project("v", 2, 2, after + 1, 0)
+
+        store_right(CHANNELS - 1, waiting[0], waiting[1], (nc.scalar.copy, nc.vector.tensor_copy))

@@ -48,22 +48,25 @@ def tile_attentionconv_kernel(tc, x, W_qkv_words, W_qkv_scales, b_qkv, out):
 
         bias_rows = keep.tile([P, P], BF16)
         nc.vector.memset(bias_rows[:], 0.0)
-        nc.scalar.dma_start(out=bias_rows[0 : 3 * E_TILES, :], in_=b_qkv.rearrange("(t p) -> t p", p=P))
+        nc.sync.dma_start(out=bias_rows[0 : 3 * E_TILES, :], in_=b_qkv.rearrange("(t p) -> t p", p=P))
 
         w_scales = keep.tile([P, PASSES, 3 * D], U8, align_bytes=64)
         nc.vector.memset(w_scales[:].rearrange("p g n -> p (g n)").bitcast(I32), 0)
         for quad in range(4):
-            nc.scalar.dma_start(
-                out=w_scales[32 * quad : 32 * quad + 4, :, :].bitcast(F32),
-                in_=W_qkv_scales[:, 4 * quad : 4 * quad + 4, :].rearrange("g r n -> r g n").bitcast(F32),
+            nc.sync.dma_start(
+                out=w_scales[32 * quad : 32 * quad + 4, :, :].bitcast(I32),
+                in_=W_qkv_scales[:, 4 * quad : 4 * quad + 4, :].rearrange("g r n -> r g n").bitcast(I32),
             )
 
         w_words = keep.tile([P, PASSES, 3 * D], U32, align_bytes=64)
-        for section in (1, 2, 0):
-            nc.sync.dma_start(
-                out=w_words[:, :, section * D : (section + 1) * D].bitcast(I32),
-                in_=W_qkv_words.rearrange("g p n t -> p g (n t)")[:, :, 4 * section * D : 4 * (section + 1) * D].bitcast(I32),
-            )
+        for first_column, last_column in ((0, D // CHANNELS), (D // CHANNELS, D)):
+            for section in (1, 2, 0):
+                nc.sync.dma_start(
+                    out=w_words[:, :, section * D + first_column : section * D + last_column].bitcast(I32),
+                    in_=W_qkv_words.rearrange("g p n t -> p g (n t)")[
+                        :, :, 4 * (section * D + first_column) : 4 * (section * D + last_column)
+                    ].bitcast(I32),
+                )
 
         p_index = keep.tile([P, 1], I32)
         nc.gpsimd.iota(p_index[:], pattern=[[0, 1]], base=0, channel_multiplier=1)
@@ -85,26 +88,6 @@ def tile_attentionconv_kernel(tc, x, W_qkv_words, W_qkv_scales, b_qkv, out):
         taps = keep.tile([P, 6], F32)
         nc.scalar.activation(out=taps[:], in_=exponents[:], func=ACT.Exp)
 
-        bias_rows_f32 = keep.tile([P, P], F32)
-        nc.scalar.copy(out=bias_rows_f32[:], in_=bias_rows[:])
-        bias_t = psum.tile([P, BANK], F32, tag="kq", bufs=4)
-        nc.tensor.transpose(bias_t[:, 0:P], bias_rows_f32[:], ident[:])
-        bias = keep.tile([P, 3 * E_TILES], F32)
-        nc.scalar.copy(out=bias[:], in_=bias_t[:, 0 : 3 * E_TILES])
-
-        edge = keep.tile([P, E_TILES], F32)
-        nc.gpsimd.tensor_tensor(out=edge[:], in0=bias[:, E_TILES : 2 * E_TILES], in1=bias[:, 2 * E_TILES : 3 * E_TILES], op=ALU.mult)
-        tap_sum = keep.tile([P, 2], F32)
-        nc.gpsimd.tensor_tensor(out=tap_sum[:], in0=taps[:, 2:4], in1=taps[:, 4:6], op=ALU.add)
-        nc.gpsimd.tensor_scalar_add(out=tap_sum[:], in0=tap_sum[:], scalar1=1.0)
-        edge_rows = keep.tile([P, E_TILES], F32)
-        nc.gpsimd.tensor_tensor(
-            out=edge_rows[:].rearrange("p (c h) -> p c h", h=2),
-            in0=edge[:].rearrange("p (c h) -> p c h", h=2),
-            in1=tap_sum[:].unsqueeze(1).to_broadcast([P, CHANNELS, 2]),
-            op=ALU.mult,
-        )
-
         x_words = x_sb[:].bitcast(F32).rearrange("p q (r j s u) -> p q u j r s", j=GRID, s=4, u=2)
         sorted_words = keep.tile([P, GRID, 2, P], F32)
         for quarter in range(QUARTERS):
@@ -116,11 +99,16 @@ def tile_attentionconv_kernel(tc, x, W_qkv_words, W_qkv_scales, b_qkv, out):
                     in_=x_words[:, quarter, u],
                 )
 
+        warm = psum.tile([P, BANK], F32, tag="kq", bufs=4)
+        for quarter, repeats in ((0, 3), (1, 3), (2, 2)):
+            for repeat in range(repeats):
+                nc.tensor.matmul(warm[:], lhsT=x_sb[:, quarter, 0:P], rhs=x_sb[:, quarter, 0:BANK], start=True, stop=True)
+
         grouped = keep.tile([P, PASSES, 4 * PATCHES], BF16, align_bytes=64)
         grouped_words = grouped[:].bitcast(F32)
         x_codes = keep.tile([P, PASSES, PATCHES], U32, align_bytes=64)
         x_scales = keep.tile([P, PASSES, PATCHES], U8, align_bytes=64)
-        for half in range(HALVES):
+        def transpose_and_quantise(half):
             for j0 in range(half * J_BANK, (half + 1) * J_BANK, 2):
                 odd = (j0 // 2) % 2
                 if odd:
@@ -141,6 +129,30 @@ def tile_attentionconv_kernel(tc, x, W_qkv_words, W_qkv_scales, b_qkv, out):
                     scales=x_scales[:, g, half * BANK : (half + 1) * BANK],
                     in_=grouped[:, g, 4 * half * BANK : 4 * (half + 1) * BANK],
                 )
+
+        transpose_and_quantise(0)
+
+        bias_rows_f32 = keep.tile([P, P], F32)
+        nc.scalar.copy(out=bias_rows_f32[:], in_=bias_rows[:])
+        bias_t = psum.tile([P, BANK], F32, tag="kq", bufs=4)
+        nc.tensor.transpose(bias_t[:, 0:P], bias_rows_f32[:], ident[:])
+        bias = keep.tile([P, 3 * E_TILES], F32)
+        nc.scalar.copy(out=bias[:], in_=bias_t[:, 0 : 3 * E_TILES])
+
+        edge = keep.tile([P, E_TILES], F32)
+        nc.gpsimd.tensor_tensor(out=edge[:], in0=bias[:, E_TILES : 2 * E_TILES], in1=bias[:, 2 * E_TILES : 3 * E_TILES], op=ALU.mult)
+        tap_sum = keep.tile([P, 2], F32)
+        nc.gpsimd.tensor_tensor(out=tap_sum[:], in0=taps[:, 2:4], in1=taps[:, 4:6], op=ALU.add)
+        nc.gpsimd.tensor_scalar_add(out=tap_sum[:], in0=tap_sum[:], scalar1=1.0)
+        edge_rows = keep.tile([P, E_TILES], F32)
+        nc.gpsimd.tensor_tensor(
+            out=edge_rows[:].rearrange("p (c h) -> p c h", h=2),
+            in0=edge[:].rearrange("p (c h) -> p c h", h=2),
+            in1=tap_sum[:].unsqueeze(1).to_broadcast([P, CHANNELS, 2]),
+            op=ALU.mult,
+        )
+
+        transpose_and_quantise(1)
 
         def project(tag, bufs, section, channel, half):
             banks = []
@@ -351,8 +363,8 @@ def tile_attentionconv_kernel(tc, x, W_qkv_words, W_qkv_scales, b_qkv, out):
                     op1=ALU.add,
                 )
             result = work.tile([P, J_BANK, P], F32, tag="result")
-            for j0 in (4, 0):
-                nc.gpsimd.tensor_tensor(
+            for j0 in (4, 0) if after < CHANNELS else (0, 4):
+                (nc.gpsimd if after < CHANNELS else nc.vector).tensor_tensor(
                     out=result[:, j0 : j0 + 4, :].rearrange("p j n -> p (j n)"),
                     in0=flat(q_sb[:, J_BANK + j0 : J_BANK + j0 + 4]),
                     in1=window[:, j0 : j0 + 4, :].rearrange("p j n -> p (j n)"),
@@ -383,4 +395,4 @@ def tile_attentionconv_kernel(tc, x, W_qkv_words, W_qkv_scales, b_qkv, out):
                 k_sbs[after + 1] = k_sb
                 v_left[after + 1] = project("v", 2, 2, after + 1, 0)
 
-        store_right(CHANNELS - 1, waiting[0], waiting[1], (nc.scalar.copy, nc.vector.tensor_copy))
+        store_right(CHANNELS - 1, waiting[0], waiting[1], (nc.scalar.copy,))

@@ -272,24 +272,24 @@ def tile_attentionconv_kernel(tc, x, W_qkv_words, W_qkv_scales, b_qkv, out):
             rows_pad = rows_pads[channel]
             q_sb = q_sbs[channel]
 
-            for upper in range(2):
+            def sum_rows(first, last, step, upper):
+                shift = (PAD - BATCH, PAD + BATCH)[step]
                 nc.vector.scalar_tensor_tensor(
-                    out=rows_pad[:, 1 : GRID + 1, :, upper, :],
-                    in0=kv_pad[:, upper, :, PAD - BATCH : PAD - BATCH + COLUMN].rearrange("p j (i b) -> p j i b", b=BATCH),
-                    scalar=taps[:, 2 + upper : 3 + upper],
-                    in1=kv_pad[:, upper, :, PAD : PAD + COLUMN].rearrange("p j (i b) -> p j i b", b=BATCH),
+                    out=rows_pad[:, first + 1 : last + 1, :, upper, :],
+                    in0=kv_pad[:, upper, first:last, shift : shift + COLUMN].rearrange("p j (i b) -> p j i b", b=BATCH),
+                    scalar=taps[:, 2 + 2 * step + upper : 3 + 2 * step + upper],
+                    in1=(
+                        kv_pad[:, upper, first:last, PAD : PAD + COLUMN].rearrange("p j (i b) -> p j i b", b=BATCH)
+                        if step == 0
+                        else rows_pad[:, first + 1 : last + 1, :, upper, :]
+                    ),
                     op0=ALU.mult,
                     op1=ALU.add,
                 )
-            for upper in range(2):
-                nc.vector.scalar_tensor_tensor(
-                    out=rows_pad[:, 1 : GRID + 1, :, upper, :],
-                    in0=kv_pad[:, upper, :, PAD + BATCH : PAD + BATCH + COLUMN].rearrange("p j (i b) -> p j i b", b=BATCH),
-                    scalar=taps[:, 4 + upper : 5 + upper],
-                    in1=rows_pad[:, 1 : GRID + 1, :, upper, :],
-                    op0=ALU.mult,
-                    op1=ALU.add,
-                )
+
+            for step in range(2):
+                for upper in range(2):
+                    sum_rows(0, J_BANK + 1, step, upper)
 
             from_left = work.tile([P, J_BANK, P], F32, tag="from_left")
             nc.scalar.activation(
@@ -299,19 +299,22 @@ def tile_attentionconv_kernel(tc, x, W_qkv_words, W_qkv_scales, b_qkv, out):
                 scale=taps[:, 0:1],
             )
             from_right = work.tile([P, J_BANK, P], F32, tag="from_right")
-            if after < CHANNELS:
-                kv_pad_after = work.tile([P, 2, GRID, PAD + COLUMN + PAD], F32, tag="kv_pad")
-                rows_pad_after = work.tile([P, GRID + 2, GRID, 2, BATCH], F32, tag="rows_pad")
-                kv_pads[after] = kv_pad_after
-                rows_pads[after] = rows_pad_after
-                multiply_kv(after, 0, 0, v_left[after], k_sbs[after], kv_pad_after)
+            sum_rows(J_BANK + 1, GRID, 0, 0)
             nc.vector.tensor_scalar_mul(
                 out=from_right[:].rearrange("p j n -> p (j n)"),
                 in0=flat(rows_pad[:, 2 : J_BANK + 2]),
                 scalar1=taps[:, 1:2],
             )
+            sum_rows(J_BANK + 1, GRID, 0, 1)
+            for upper in range(2):
+                sum_rows(J_BANK + 1, GRID, 1, upper)
             if after < CHANNELS:
-                multiply_kv(after, 0, 1, v_left[after], k_sbs[after], kv_pad_after)
+                kv_pad_after = work.tile([P, 2, GRID, PAD + COLUMN + PAD], F32, tag="kv_pad")
+                rows_pad_after = work.tile([P, GRID + 2, GRID, 2, BATCH], F32, tag="rows_pad")
+                kv_pads[after] = kv_pad_after
+                rows_pads[after] = rows_pad_after
+                for upper in range(2):
+                    multiply_kv(after, 0, upper, v_left[after], k_sbs[after], kv_pad_after)
 
             if waiting is not None:
                 store_right(channel - 1, waiting[0], waiting[1], (nc.scalar.copy,))

@@ -154,23 +154,25 @@ def tile_attentionconv_kernel(tc, x, W_qkv_words, W_qkv_scales, b_qkv, out):
 
         transpose_and_quantise(1)
 
+        def project_tile(tag, bufs, section, channel, half, upper):
+            acc = psum.tile([P, BANK], F32, tag=tag, bufs=bufs)
+            first = section * D + (2 * channel + upper) * P
+            for g in range(PASSES):
+                nc.tensor.matmul_mx(
+                    out=acc[:],
+                    lhsT=w_words[:, g, first : first + P].bitcast(FP8X4),
+                    lhsT_scale=w_scales[:, g, first : first + P],
+                    rhs=x_codes[:, g, half * BANK : (half + 1) * BANK].bitcast(FP8X4),
+                    rhs_scale=x_scales[:, g, half * BANK : (half + 1) * BANK],
+                    start=(g == 0),
+                    stop=(g == PASSES - 1),
+                )
+            return acc
+
         def project(tag, bufs, section, channel, half):
-            banks = []
-            for upper in range(2):
-                acc = psum.tile([P, BANK], F32, tag=tag, bufs=bufs)
-                first = section * D + (2 * channel + upper) * P
-                for g in range(PASSES):
-                    nc.tensor.matmul_mx(
-                        out=acc[:],
-                        lhsT=w_words[:, g, first : first + P].bitcast(FP8X4),
-                        lhsT_scale=w_scales[:, g, first : first + P],
-                        rhs=x_codes[:, g, half * BANK : (half + 1) * BANK].bitcast(FP8X4),
-                        rhs_scale=x_scales[:, g, half * BANK : (half + 1) * BANK],
-                        start=(g == 0),
-                        stop=(g == PASSES - 1),
-                    )
-                banks.append(acc)
-            return banks
+            lower_tile = project_tile(tag, bufs, section, channel, half, 0)
+            upper_tile = project_tile(tag, bufs, section, channel, half, 1)
+            return [lower_tile, upper_tile]
 
         def bias_of(section, channel, upper):
             column = section * E_TILES + 2 * channel + upper
@@ -187,17 +189,16 @@ def tile_attentionconv_kernel(tc, x, W_qkv_words, W_qkv_scales, b_qkv, out):
                     scale=1.0,
                 )
 
-        def project_q(channel, q_sb):
-            for half in range(HALVES):
-                q_ps = project("kq", 4, 0, channel, half)
-                for upper in range(2):
-                    nc.scalar.activation(
-                        out=q_sb[:, half * J_BANK : (half + 1) * J_BANK, :, upper, :],
-                        in_=q_ps[upper][:].rearrange("p (j i b) -> p j i b", i=GRID, b=BATCH),
-                        func=ACT.Identity,
-                        bias=bias_of(0, channel, upper),
-                        scale=1.0,
-                    )
+        def project_q(channel, half, q_sb):
+            q_ps = project("kq", 4, 0, channel, half)
+            for upper in range(2):
+                nc.scalar.activation(
+                    out=q_sb[:, half * J_BANK : (half + 1) * J_BANK, :, upper, :],
+                    in_=q_ps[upper][:].rearrange("p (j i b) -> p j i b", i=GRID, b=BATCH),
+                    func=ACT.Identity,
+                    bias=bias_of(0, channel, upper),
+                    scale=1.0,
+                )
 
         def borders(channel, kv_pad, rows_pad):
             for upper in range(2):
@@ -257,7 +258,8 @@ def tile_attentionconv_kernel(tc, x, W_qkv_words, W_qkv_scales, b_qkv, out):
         kv_pads[0] = kv_pad
         rows_pads[0] = rows_pad
         q_sb = work.tile([P, GRID, GRID, 2, BATCH], F32, tag="q_sb")
-        project_q(0, q_sb)
+        for half in range(HALVES):
+            project_q(0, half, q_sb)
         q_sbs[0] = q_sb
         k_sb = work.tile([P, 2, PATCHES], F32, tag="k_sb")
         for half in range(HALVES):
@@ -313,8 +315,7 @@ def tile_attentionconv_kernel(tc, x, W_qkv_words, W_qkv_scales, b_qkv, out):
                 rows_pad_after = work.tile([P, GRID + 2, GRID, 2, BATCH], F32, tag="rows_pad")
                 kv_pads[after] = kv_pad_after
                 rows_pads[after] = rows_pad_after
-                for upper in range(2):
-                    multiply_kv(after, 0, upper, v_left[after], k_sbs[after], kv_pad_after)
+                multiply_kv(after, 0, 0, v_left[after], k_sbs[after], kv_pad_after)
 
             if waiting is not None:
                 store_right(channel - 1, waiting[0], waiting[1], (nc.scalar.copy,))
@@ -374,6 +375,9 @@ def tile_attentionconv_kernel(tc, x, W_qkv_words, W_qkv_scales, b_qkv, out):
                     op=ALU.mult,
                 )
 
+            if after < CHANNELS:
+                multiply_kv(after, 0, 1, v_left[after], k_sbs[after], kv_pad_after)
+
             image_rows = work.tile([P, PATCH // 2, GRID, PATCH], F32, tag="image_rows")
             for j0 in range(0, J_BANK, 4):
                 nc.vector.tensor_tensor(
@@ -385,12 +389,14 @@ def tile_attentionconv_kernel(tc, x, W_qkv_words, W_qkv_scales, b_qkv, out):
             waiting = (result, image_rows)
 
             if after < CHANNELS:
-                v_right = project("v", 2, 2, after, 1)
-                for upper in range(2):
-                    multiply_kv(after, 1, upper, v_right, k_sbs[after], kv_pad_after)
                 q_sb_after = work.tile([P, GRID, GRID, 2, BATCH], F32, tag="q_sb")
-                project_q(after, q_sb_after)
                 q_sbs[after] = q_sb_after
+                v_right_lower = project_tile("v", 2, 2, after, 1, 0)
+                project_q(after, 0, q_sb_after)
+                v_right_upper = project_tile("v", 2, 2, after, 1, 1)
+                for upper in range(2):
+                    multiply_kv(after, 1, upper, [v_right_lower, v_right_upper], k_sbs[after], kv_pad_after)
+                project_q(after, 1, q_sb_after)
             if after + 1 < CHANNELS:
                 k_sb = work.tile([P, 2, PATCHES], F32, tag="k_sb")
                 for half in range(HALVES):

@@ -301,12 +301,21 @@ def tile_attentionconv_kernel(tc, x, W_qkv_words, W_qkv_scales, b_qkv, out):
                 scale=taps[:, 0:1],
             )
             from_right = work.tile([P, J_BANK, P], F32, tag="from_right")
-            sum_rows(J_BANK + 1, GRID, 0, 0)
-            nc.vector.tensor_scalar_mul(
-                out=from_right[:].rearrange("p j n -> p (j n)"),
-                in0=flat(rows_pad[:, 2 : J_BANK + 2]),
-                scalar1=taps[:, 1:2],
-            )
+            if after + 1 < CHANNELS:
+                sum_rows(J_BANK + 1, GRID, 0, 0)
+                nc.vector.tensor_scalar_mul(
+                    out=from_right[:].rearrange("p j n -> p (j n)"),
+                    in0=flat(rows_pad[:, 2 : J_BANK + 2]),
+                    scalar1=taps[:, 1:2],
+                )
+            else:
+                nc.scalar.activation(
+                    out=from_right[:].rearrange("p j n -> p (j n)"),
+                    in_=flat(rows_pad[:, 2 : J_BANK + 2]),
+                    func=ACT.Identity,
+                    scale=taps[:, 1:2],
+                )
+                sum_rows(J_BANK + 1, GRID, 0, 0)
             sum_rows(J_BANK + 1, GRID, 0, 1)
             for upper in range(2):
                 sum_rows(J_BANK + 1, GRID, 1, upper)

@@ -336,6 +336,11 @@ def tile_attentionconv_kernel(tc, x, W_qkv_words, W_qkv_scales, b_qkv, out):
                     nc.tensor.transpose(q_t[:, jl, :], q_sb[:, j0 + jl].rearrange("p i h b -> p (i h b)"), ident[:])
                 nc.scalar.copy(out=q_t_sb[:, j0 : j0 + 4, :], in_=q_t[:])
 
+            if after == CHANNELS:
+                idle = psum.tile([P, BANK], F32, tag="v", bufs=2)
+                for repeat in range(10):
+                    nc.tensor.matmul(idle[:], lhsT=x_sb[:, 0, 0:P], rhs=x_sb[:, 0, 0:BANK], start=True, stop=True)
+
             sums = []
             for j0 in range(0, J_BANK, 4):
                 sum_t = psum.tile([P, 4, P], F32, tag="sum", bufs=2)

@@ -50,12 +50,12 @@ def tile_attentionconv_kernel(tc, x, W_qkv_words, W_qkv_scales, b_qkv, out):
         nc.vector.memset(bias_rows[:], 0.0)
         nc.sync.dma_start(out=bias_rows[0 : 3 * E_TILES, :], in_=b_qkv.rearrange("(t p) -> t p", p=P))
 
-        w_scales = keep.tile([P, PASSES, 3 * D], U8, align_bytes=64)
-        nc.vector.memset(w_scales[:].rearrange("p g n -> p (g n)").bitcast(I32), 0)
+        w_scales = keep.tile([P, 3 * D], U8, align_bytes=64)
+        nc.vector.memset(w_scales[:].bitcast(I32), 0)
         for quad in range(4):
             nc.sync.dma_start(
-                out=w_scales[32 * quad : 32 * quad + 4, :, :].bitcast(I32),
-                in_=W_qkv_scales[:, 4 * quad : 4 * quad + 4, :].rearrange("g r n -> r g n").bitcast(I32),
+                out=w_scales[32 * quad : 32 * quad + 4 * PASSES, :].bitcast(I32),
+                in_=W_qkv_scales[:, 4 * quad : 4 * quad + 4, :].bitcast(I32),
             )
 
         w_words = keep.tile([P, PASSES, 3 * D], U32, align_bytes=64)
@@ -161,7 +161,7 @@ def tile_attentionconv_kernel(tc, x, W_qkv_words, W_qkv_scales, b_qkv, out):
                 nc.tensor.matmul_mx(
                     out=acc[:],
                     lhsT=w_words[:, g, first : first + P].bitcast(FP8X4),
-                    lhsT_scale=w_scales[:, g, first : first + P],
+                    lhsT_scale=w_scales[4 * g : P, first : first + P],
                     rhs=x_codes[:, g, half * BANK : (half + 1) * BANK].bitcast(FP8X4),
                     rhs_scale=x_scales[:, g, half * BANK : (half + 1) * BANK],
                     start=(g == 0),

@@ -174,6 +174,21 @@ def tile_attentionconv_kernel(tc, x, W_qkv_words, W_qkv_scales, b_qkv, out):
             upper_tile = project_tile(tag, bufs, section, channel, half, 1)
             return [lower_tile, upper_tile]
 
+        def project_kv(channel, half, tag):
+            v_tiles = []
+            for upper in range(2):
+                k_ps = project_tile("kq", 4, 1, channel, half, upper)
+                nc.scalar.activation(
+                    out=k_sbs[channel][:, upper, half * BANK : (half + 1) * BANK],
+                    in_=k_ps[:],
+                    func=ACT.Identity,
+                    bias=bias_of(1, channel, upper),
+                    scale=1.0,
+                )
+                v_tile = project_tile(tag, 2, 2, channel, half, upper)
+                v_tiles.append(v_tile)
+            v_banks[channel, half] = v_tiles
+
         def bias_of(section, channel, upper):
             column = section * E_TILES + 2 * channel + upper
             return bias[:, column : column + 1]
@@ -227,139 +242,149 @@ def tile_attentionconv_kernel(tc, x, W_qkv_words, W_qkv_scales, b_qkv, out):
 
         out_rows = out.rearrange("b c (m r) w -> c m b (r w)", r=PATCH // 2)
 
-        def store_right(channel, result, image_rows, copies):
-            for j0 in range(0, J_BANK, 4):
-                out_t = psum.tile([P, 4, P], F32, tag="kq", bufs=4)
-                for jl in range(4):
-                    nc.tensor.transpose(out_t[:, jl, :], result[:, j0 + jl, :], ident[:])
-                copies[(j0 // 4) % len(copies)](
-                    out=image_rows[:, :, J_BANK + j0 : J_BANK + j0 + 4, :],
-                    in_=out_t[:].rearrange("p j (r s) -> p r j s", s=PATCH),
-                )
-            nc.sync.dma_start(out=out_rows[channel], in_=image_rows[:].rearrange("p r j s -> p (r j s)"))
 
         k_sbs = {}
-        v_left = {}
+        v_banks = {}
         kv_pads = {}
         rows_pads = {}
         q_sbs = {}
-        k_sb = work.tile([P, 2, PATCHES], F32, tag="k_sb")
-        kv_pad = work.tile([P, 2, GRID, PAD + COLUMN + PAD], F32, tag="kv_pad")
-        rows_pad = work.tile([P, GRID + 2, GRID, 2, BATCH], F32, tag="rows_pad")
-        project_k(0, 0, k_sb)
-        v_ps0 = project("v", 2, 2, 0, 0)
-        project_k(0, 1, k_sb)
-        v_ps1 = project("sum", 2, 2, 0, 1)
-        borders(0, kv_pad, rows_pad)
-        for upper in range(2):
-            multiply_kv(0, 0, upper, v_ps0, k_sb, kv_pad)
-        for upper in range(2):
-            multiply_kv(0, 1, upper, v_ps1, k_sb, kv_pad)
-        kv_pads[0] = kv_pad
-        rows_pads[0] = rows_pad
-        q_sb = work.tile([P, GRID, GRID, 2, BATCH], F32, tag="q_sb")
-        for half in range(HALVES):
-            project_q(0, half, q_sb)
-        q_sbs[0] = q_sb
-        k_sb = work.tile([P, 2, PATCHES], F32, tag="k_sb")
-        for half in range(HALVES):
-            project_k(1, half, k_sb)
-        k_sbs[1] = k_sb
-        v_left[1] = project("v", 2, 2, 1, 0)
 
-        waiting = None
-        for channel in range(CHANNELS):
-            after = channel + 1
+        def start_channel(channel):
+            k_sb = work.tile([P, 2, PATCHES], F32, tag="k_sb")
+            kv_pad = work.tile([P, 2, GRID, PAD + COLUMN + PAD], F32, tag="kv_pad")
+            rows_pad = work.tile([P, GRID + 2, GRID, 2, BATCH], F32, tag="rows_pad")
+            k_sbs[channel] = k_sb
+            kv_pads[channel] = kv_pad
+            rows_pads[channel] = rows_pad
+
+        start_channel(0)
+        project_k(0, 0, k_sbs[0])
+        borders(0, kv_pads[0], rows_pads[0])
+        v_banks[0, 0] = project("v", 2, 2, 0, 0)
+        project_k(0, 1, k_sbs[0])
+        v_banks[0, 1] = project("sum", 2, 2, 0, 1)
+        for upper in range(2):
+            multiply_kv(0, 0, upper, v_banks[0, 0], k_sbs[0], kv_pads[0])
+
+        def sum_rows(channel, first, end, step, upper):
             kv_pad = kv_pads[channel]
             rows_pad = rows_pads[channel]
-            q_sb = q_sbs[channel]
+            shift = (PAD - BATCH, PAD + BATCH)[step]
+            nc.vector.scalar_tensor_tensor(
+                out=rows_pad[:, first + 1 : end + 1, :, upper, :],
+                in0=kv_pad[:, upper, first:end, shift : shift + COLUMN].rearrange("p j (i b) -> p j i b", b=BATCH),
+                scalar=taps[:, 2 + 2 * step + upper : 3 + 2 * step + upper],
+                in1=(
+                    kv_pad[:, upper, first:end, PAD : PAD + COLUMN].rearrange("p j (i b) -> p j i b", b=BATCH)
+                    if step == 0
+                    else rows_pad[:, first + 1 : end + 1, :, upper, :]
+                ),
+                op0=ALU.mult,
+                op1=ALU.add,
+            )
 
-            def sum_rows(first, last, step, upper):
-                shift = (PAD - BATCH, PAD + BATCH)[step]
-                nc.vector.scalar_tensor_tensor(
-                    out=rows_pad[:, first + 1 : last + 1, :, upper, :],
-                    in0=kv_pad[:, upper, first:last, shift : shift + COLUMN].rearrange("p j (i b) -> p j i b", b=BATCH),
-                    scalar=taps[:, 2 + 2 * step + upper : 3 + 2 * step + upper],
-                    in1=(
-                        kv_pad[:, upper, first:last, PAD : PAD + COLUMN].rearrange("p j (i b) -> p j i b", b=BATCH)
-                        if step == 0
-                        else rows_pad[:, first + 1 : last + 1, :, upper, :]
-                    ),
-                    op0=ALU.mult,
-                    op1=ALU.add,
-                )
-
-            for step in range(2):
-                for upper in range(2):
-                    sum_rows(0, J_BANK + 1, step, upper)
-
-            from_left = work.tile([P, J_BANK, P], F32, tag="from_left")
+        def scale_left(channel, scaled, first, end, base):
             nc.scalar.activation(
-                out=from_left[:].rearrange("p j n -> p (j n)"),
-                in_=flat(rows_pad[:, 0:J_BANK]),
+                out=scaled[:, first - base : end - base, :].rearrange("p j n -> p (j n)"),
+                in_=flat(rows_pads[channel][:, first:end]),
                 func=ACT.Identity,
                 scale=taps[:, 0:1],
             )
-            from_right = work.tile([P, J_BANK, P], F32, tag="from_right")
-            if after + 1 < CHANNELS:
-                sum_rows(J_BANK + 1, GRID, 0, 0)
-                nc.vector.tensor_scalar_mul(
-                    out=from_right[:].rearrange("p j n -> p (j n)"),
-                    in0=flat(rows_pad[:, 2 : J_BANK + 2]),
-                    scalar1=taps[:, 1:2],
-                )
-            else:
-                nc.scalar.activation(
-                    out=from_right[:].rearrange("p j n -> p (j n)"),
-                    in_=flat(rows_pad[:, 2 : J_BANK + 2]),
-                    func=ACT.Identity,
-                    scale=taps[:, 1:2],
-                )
-                sum_rows(J_BANK + 1, GRID, 0, 0)
-            sum_rows(J_BANK + 1, GRID, 0, 1)
-            for upper in range(2):
-                sum_rows(J_BANK + 1, GRID, 1, upper)
-            if after < CHANNELS:
-                kv_pad_after = work.tile([P, 2, GRID, PAD + COLUMN + PAD], F32, tag="kv_pad")
-                rows_pad_after = work.tile([P, GRID + 2, GRID, 2, BATCH], F32, tag="rows_pad")
-                kv_pads[after] = kv_pad_after
-                rows_pads[after] = rows_pad_after
-                multiply_kv(after, 0, 0, v_left[after], k_sbs[after], kv_pad_after)
 
-            if waiting is not None:
-                store_right(channel - 1, waiting[0], waiting[1], (nc.scalar.copy,))
+        def scale_right(channel, scaled, first, end, base, on_vector):
+            target = scaled[:, first - base : end - base, :].rearrange("p j n -> p (j n)")
+            source = flat(rows_pads[channel][:, first + 2 : end + 2])
+            if on_vector:
+                nc.vector.tensor_scalar_mul(out=target, in0=source, scalar1=taps[:, 1:2])
+            else:
+                nc.scalar.activation(out=target, in_=source, func=ACT.Identity, scale=taps[:, 1:2])
+
+        def transpose_q(channel, first):
+            q_t = psum.tile([P, 4, P], F32, tag="kq", bufs=4)
+            for jl in range(4):
+                nc.tensor.transpose(q_t[:, jl, :], q_sbs[channel][:, first + jl].rearrange("p i h b -> p (i h b)"), ident[:])
+            return q_t
+
+        def transpose_right(result, j0):
+            out_t = psum.tile([P, 4, P], F32, tag="kq", bufs=4)
+            for jl in range(4):
+                nc.tensor.transpose(out_t[:, jl, :], result[:, j0 + jl, :], ident[:])
+            return out_t
+
+        def fetch_right(out_t, image_rows, j0):
+            nc.scalar.copy(
+                out=image_rows[:, :, J_BANK + j0 : J_BANK + j0 + 4, :],
+                in_=out_t[:].rearrange("p j (r s) -> p r j s", s=PATCH),
+            )
+
+        def sum_columns(channel, tag, from_left, from_right, first, base, warm_ups=0):
+            rows_pad = rows_pads[channel]
+            sum_t = psum.tile([P, 4, P], F32, tag=tag, bufs=2)
+            for repeat in range(warm_ups):
+                nc.tensor.matmul(
+                    sum_t[:].rearrange("p j n -> p (j n)"), lhsT=x_sb[:, 0, 0:P], rhs=x_sb[:, 0, 0:BANK], start=True, stop=True
+                )
+            for j in range(first, first + 4):
+                columns = sum_t[:, j - first, :]
+                nc.tensor.matmul(columns, lhsT=from_left[:, j - base, :], rhs=ident[:], start=True, stop=False, is_transpose=True)
+                nc.tensor.matmul(
+                    columns,
+                    lhsT=rows_pad[:, j + 1].rearrange("p i h b -> p (i h b)"),
+                    rhs=ident[:],
+                    start=False,
+                    stop=False,
+                    is_transpose=True,
+                )
+                nc.tensor.matmul(columns, lhsT=from_right[:, j - base, :], rhs=ident[:], start=False, stop=True, is_transpose=True)
+            return sum_t
+
+        def multiply_q(sum_t, q_t_sb, image_rows, first, base):
+            nc.vector.tensor_tensor(
+                out=image_rows[:, :, first : first + 4, :],
+                in0=sum_t[:].rearrange("p j (r s) -> p r j s", s=PATCH),
+                in1=q_t_sb[:, first - base : first - base + 4, :].rearrange("p j (r s) -> p r j s", s=PATCH),
+                op=ALU.mult,
+            )
+
+        waiting = None
+        for channel in range(CHANNELS - 1):
+            after = channel + 1
+            rows_pad = rows_pads[channel]
+            q_sb = work.tile([P, GRID, GRID, 2, BATCH], F32, tag="q_sb")
+            q_sbs[channel] = q_sb
+            for half in range(HALVES):
+                project_q(channel, half, q_sb)
+
+            for step in range(2):
+                for upper in range(2):
+                    sum_rows(channel, 0, J_BANK, step, upper)
+            from_left = work.tile([P, J_BANK, P], F32, tag="from_left")
+            scale_left(channel, from_left, 0, J_BANK, 0)
+            for upper in range(2):
+                multiply_kv(channel, 1, upper, v_banks[channel, 1], k_sbs[channel], kv_pads[channel])
+            for step in range(2):
+                for upper in range(2):
+                    sum_rows(channel, J_BANK, GRID, step, upper)
+            from_right = work.tile([P, J_BANK, P], F32, tag="from_right")
+            scale_right(channel, from_right, 0, J_BANK, 0, True)
+
+            start_channel(after)
+            project_k(after, 0, k_sbs[after])
+            v_banks[after, 0] = project("v", 2, 2, after, 0)
 
             q_t_sb = work.tile([P, J_BANK, P], F32, tag="q_t_sb")
-            for j0 in range(0, J_BANK, 4):
-                q_t = psum.tile([P, 4, P], F32, tag="kq", bufs=4)
-                for jl in range(4):
-                    nc.tensor.transpose(q_t[:, jl, :], q_sb[:, j0 + jl].rearrange("p i h b -> p (i h b)"), ident[:])
-                nc.scalar.copy(out=q_t_sb[:, j0 : j0 + 4, :], in_=q_t[:])
-
-            if after == CHANNELS:
-                idle = psum.tile([P, BANK], F32, tag="v", bufs=2)
-                for repeat in range(10):
-                    nc.tensor.matmul(idle[:], lhsT=x_sb[:, 0, 0:P], rhs=x_sb[:, 0, 0:BANK], start=True, stop=True)
-
+            for first in range(0, J_BANK, 4):
+                q_t = transpose_q(channel, first)
+                nc.scalar.copy(out=q_t_sb[:, first : first + 4, :], in_=q_t[:])
+            if waiting is not None:
+                for j0 in range(0, J_BANK, 4):
+                    fetch_right(transpose_right(waiting[0], j0), waiting[1], j0)
+                nc.sync.dma_start(out=out_rows[channel - 1], in_=waiting[1][:].rearrange("p r j s -> p (r j s)"))
             sums = []
-            for j0 in range(0, J_BANK, 4):
-                sum_t = psum.tile([P, 4, P], F32, tag="sum", bufs=2)
-                for jl in range(4):
-                    j = j0 + jl
-                    nc.tensor.matmul(sum_t[:, jl, :], lhsT=from_left[:, j, :], rhs=ident[:], start=True, stop=False, is_transpose=True)
-                    nc.tensor.matmul(
-                        sum_t[:, jl, :],
-                        lhsT=rows_pad[:, j + 1].rearrange("p i h b -> p (i h b)"),
-                        rhs=ident[:],
-                        start=False,
-                        stop=False,
-                        is_transpose=True,
-                    )
-                    nc.tensor.matmul(sum_t[:, jl, :], lhsT=from_right[:, j, :], rhs=ident[:], start=False, stop=True, is_transpose=True)
-                sums.append(sum_t)
+            for first in range(0, J_BANK, 4):
+                sums.append(sum_columns(channel, "sum", from_left, from_right, first, 0, 0))
 
-            if after < CHANNELS:
-                borders(after, kv_pad_after, rows_pad_after)
+            borders(after, kv_pads[after], rows_pads[after])
 
             window = work.tile([P, J_BANK, P], F32, tag="window")
             for j0 in range(0, J_BANK, 4):
@@ -381,41 +406,96 @@ def tile_attentionconv_kernel(tc, x, W_qkv_words, W_qkv_scales, b_qkv, out):
                     op1=ALU.add,
                 )
             result = work.tile([P, J_BANK, P], F32, tag="result")
-            for j0 in (4, 0) if after < CHANNELS else (0, 4):
-                (nc.gpsimd if after < CHANNELS else nc.vector).tensor_tensor(
+            for j0 in range(0, J_BANK, 4):
+                nc.gpsimd.tensor_tensor(
                     out=result[:, j0 : j0 + 4, :].rearrange("p j n -> p (j n)"),
                     in0=flat(q_sb[:, J_BANK + j0 : J_BANK + j0 + 4]),
                     in1=window[:, j0 : j0 + 4, :].rearrange("p j n -> p (j n)"),
                     op=ALU.mult,
                 )
 
-            if after < CHANNELS:
-                multiply_kv(after, 0, 1, v_left[after], k_sbs[after], kv_pad_after)
-
+            for upper in range(2):
+                multiply_kv(after, 0, upper, v_banks[after, 0], k_sbs[after], kv_pads[after])
             image_rows = work.tile([P, PATCH // 2, GRID, PATCH], F32, tag="image_rows")
-            for j0 in range(0, J_BANK, 4):
-                nc.vector.tensor_tensor(
-                    out=image_rows[:, :, j0 : j0 + 4, :],
-                    in0=sums[j0 // 4][:].rearrange("p j (r s) -> p r j s", s=PATCH),
-                    in1=q_t_sb[:, j0 : j0 + 4, :].rearrange("p j (r s) -> p r j s", s=PATCH),
-                    op=ALU.mult,
-                )
+            for first in range(0, J_BANK, 4):
+                multiply_q(sums[first // 4], q_t_sb, image_rows, first, 0)
             waiting = (result, image_rows)
 
-            if after < CHANNELS:
-                q_sb_after = work.tile([P, GRID, GRID, 2, BATCH], F32, tag="q_sb")
-                q_sbs[after] = q_sb_after
-                v_right_lower = project_tile("v", 2, 2, after, 1, 0)
-                project_q(after, 0, q_sb_after)
-                v_right_upper = project_tile("v", 2, 2, after, 1, 1)
-                for upper in range(2):
-                    multiply_kv(after, 1, upper, [v_right_lower, v_right_upper], k_sbs[after], kv_pad_after)
-                project_q(after, 1, q_sb_after)
-            if after + 1 < CHANNELS:
-                k_sb = work.tile([P, 2, PATCHES], F32, tag="k_sb")
-                for half in range(HALVES):
-                    project_k(after + 1, half, k_sb)
-                k_sbs[after + 1] = k_sb
-                v_left[after + 1] = project("v", 2, 2, after + 1, 0)
+            project_k(after, 1, k_sbs[after])
+            v_banks[after, 1] = project("v", 2, 2, after, 1)
 
-        store_right(CHANNELS - 1, waiting[0], waiting[1], (nc.scalar.copy,))
+        channel = CHANNELS - 1
+        q_sb = work.tile([P, GRID, GRID, 2, BATCH], F32, tag="q_sb")
+        q_sbs[channel] = q_sb
+        image_rows = work.tile([P, PATCH // 2, GRID, PATCH], F32, tag="image_rows")
+        halves = []
+        for half in range(HALVES):
+            from_left = work.tile([P, J_BANK, P], F32, tag="from_left")
+            from_right = work.tile([P, J_BANK, P], F32, tag="from_right")
+            q_t_sb = work.tile([P, J_BANK, P], F32, tag="q_t_sb")
+            halves.append((from_left, from_right, q_t_sb))
+
+        def quad(first):
+            return halves[first // J_BANK] + (first // J_BANK * J_BANK,)
+
+        def fetch_q(q_t, first):
+            nc.scalar.copy(out=quad(first)[2][:, first - quad(first)[3] : first - quad(first)[3] + 4, :], in_=q_t[:])
+
+        def rows(first, end):
+            for step in range(2):
+                for upper in range(2):
+                    sum_rows(channel, first, end, step, upper)
+
+        def quad_left(first):
+            scale_left(channel, quad(first)[0], first, first + 4, quad(first)[3])
+
+        def quad_right(first):
+            scale_right(channel, quad(first)[1], first, first + 4, quad(first)[3], True)
+
+        sums = {}
+
+        def quad_sum(first):
+            from_left, from_right, q_t_sb, base = quad(first)
+            sums[first] = sum_columns(channel, ("sum", "v")[first // J_BANK], from_left, from_right, first, base)
+
+        def quad_multiply(first):
+            multiply_q(sums[first], quad(first)[2], image_rows, first, quad(first)[3])
+
+        for half in range(HALVES):
+            project_q(channel, half, q_sb)
+        right_0 = transpose_right(waiting[0], 0)
+        right_4 = transpose_right(waiting[0], 4)
+        q_0 = transpose_q(channel, 0)
+        q_4 = transpose_q(channel, 4)
+        rows(0, 5)
+        quad_left(0)
+        quad_right(0)
+        quad_sum(0)
+        fetch_right(right_0, waiting[1], 0)
+        fetch_right(right_4, waiting[1], 4)
+        nc.sync.dma_start(out=out_rows[channel - 1], in_=waiting[1][:].rearrange("p r j s -> p (r j s)"))
+        rows(5, J_BANK)
+        quad_left(4)
+        q_8 = transpose_q(channel, 8)
+        for upper in range(2):
+            multiply_kv(channel, 1, upper, v_banks[channel, 1], k_sbs[channel], kv_pads[channel])
+        rows(J_BANK, 13)
+        quad_right(4)
+        quad_right(8)
+        quad_left(8)
+        quad_sum(4)
+        quad_sum(8)
+        fetch_q(q_0, 0)
+        rows(13, GRID)
+        quad_right(12)
+        quad_left(12)
+        q_12 = transpose_q(channel, 12)
+        quad_sum(12)
+        fetch_q(q_4, 4)
+        fetch_q(q_8, 8)
+        fetch_q(q_12, 12)
+        quad_multiply(0)
+        quad_multiply(4)
+        quad_multiply(8)
+        quad_multiply(12)
+        nc.sync.dma_start(out=out_rows[channel], in_=image_rows[:].rearrange("p r j s -> p (r j s)"))

@@ -41,6 +41,11 @@ def tile_attentionconv_kernel(tc, x, W_qkv_words, W_qkv_scales, b_qkv, out):
         work = ctx.enter_context(tc.tile_pool(name="work", bufs=2))
         psum = ctx.enter_context(tc.psum_pool(name="psum", bufs=4))
 
+        p_index = keep.tile([P, 1], I32)
+        nc.gpsimd.iota(p_index[:], pattern=[[0, 1]], base=0, channel_multiplier=1)
+        ident = keep.tile([P, P], F32)
+        make_identity(nc, ident[:])
+
         x_rows = x.rearrange("b (g c) (i q r) w -> c q i (b g) (r w)", g=2, c=2, i=GRID, q=2)
         x_sb = keep.tile([P, QUARTERS, PATCH // 2 * WIDTH], BF16)
         for quarter in range(QUARTERS):
@@ -48,14 +53,14 @@ def tile_attentionconv_kernel(tc, x, W_qkv_words, W_qkv_scales, b_qkv, out):
 
         bias_rows = keep.tile([P, P], BF16)
         nc.vector.memset(bias_rows[:], 0.0)
-        nc.sync.dma_start(out=bias_rows[0 : 3 * E_TILES, :], in_=b_qkv.rearrange("(t p) -> t p", p=P))
+        nc.gpsimd.dma_start(out=bias_rows[0 : 3 * E_TILES, :], in_=b_qkv.rearrange("(t p) -> t p", p=P))
 
         w_scales = keep.tile([P, 3 * D], U8, align_bytes=64)
         nc.vector.memset(w_scales[:].bitcast(I32), 0)
         for quad in range(4):
-            nc.sync.dma_start(
-                out=w_scales[32 * quad : 32 * quad + 4 * PASSES, :].bitcast(I32),
-                in_=W_qkv_scales[:, 4 * quad : 4 * quad + 4, :].bitcast(I32),
+            nc.gpsimd.dma_start(
+                out=w_scales[32 * quad : 32 * quad + 4 * PASSES, :].bitcast(F32),
+                in_=W_qkv_scales[:, 4 * quad : 4 * quad + 4, :].bitcast(F32),
             )
 
         w_words = keep.tile([P, PASSES, 3 * D], U32, align_bytes=64)
@@ -68,10 +73,6 @@ def tile_attentionconv_kernel(tc, x, W_qkv_words, W_qkv_scales, b_qkv, out):
                     ].bitcast(I32),
                 )
 
-        p_index = keep.tile([P, 1], I32)
-        nc.gpsimd.iota(p_index[:], pattern=[[0, 1]], base=0, channel_multiplier=1)
-        ident = keep.tile([P, P], F32)
-        make_identity(nc, ident[:])
         rs_int = keep.tile([P, 2], I32)
         nc.vector.tensor_single_scalar(out=rs_int[:, 0:1], in_=p_index[:], scalar=PATCH - 1, op=ALU.bitwise_and)
         nc.vector.tensor_single_scalar(out=rs_int[:, 1:2], in_=p_index[:], scalar=4, op=ALU.logical_shift_right)
@@ -88,16 +89,23 @@ def tile_attentionconv_kernel(tc, x, W_qkv_words, W_qkv_scales, b_qkv, out):
         taps = keep.tile([P, 6], F32)
         nc.scalar.activation(out=taps[:], in_=exponents[:], func=ACT.Exp)
 
+        bias_rows_f32 = keep.tile([P, P], F32)
         x_words = x_sb[:].bitcast(F32).rearrange("p q (r j s u) -> p q u j r s", j=GRID, s=4, u=2)
         sorted_words = keep.tile([P, GRID, 2, P], F32)
         for quarter in range(QUARTERS):
-            for u in range(2):
-                nc.vector.tensor_copy(
-                    out=sorted_words[:, :, u, quarter * P // QUARTERS : (quarter + 1) * P // QUARTERS].rearrange(
-                        "p j (r s) -> p j r s", s=4
-                    ),
-                    in_=x_words[:, quarter, u],
-                )
+            shares = ((nc.vector.tensor_copy, 0, GRID),)
+            if quarter == QUARTERS - 1:
+                shares = ((nc.vector.tensor_copy, 0, J_BANK), (nc.scalar.copy, J_BANK, GRID))
+            for copy, first, end in shares:
+                for u in range(2):
+                    copy(
+                        out=sorted_words[:, first:end, u, quarter * P // QUARTERS : (quarter + 1) * P // QUARTERS].rearrange(
+                            "p j (r s) -> p j r s", s=4
+                        ),
+                        in_=x_words[:, quarter, u, first:end],
+                    )
+
+        nc.scalar.copy(out=bias_rows_f32[:], in_=bias_rows[:])
 
         warm = psum.tile([P, BANK], F32, tag="kq", bufs=4)
         for quarter, repeats in ((0, 3), (1, 3), (2, 2)):
@@ -110,7 +118,7 @@ def tile_attentionconv_kernel(tc, x, W_qkv_words, W_qkv_scales, b_qkv, out):
         x_scales = keep.tile([P, PASSES, PATCHES], U8, align_bytes=64)
         def transpose_and_quantise(half):
             for j0 in range(half * J_BANK, (half + 1) * J_BANK, 2):
-                odd = (j0 // 2) % 2
+                odd = (j0 // 2) % 2 and j0 != 10
                 if odd:
                     x_t = psum.tile([P, 2, 2 * P], F32, tag=("v" if (j0 // 4) % 2 == 0 else "sum"), bufs=2)
                 else:
@@ -132,8 +140,6 @@ def tile_attentionconv_kernel(tc, x, W_qkv_words, W_qkv_scales, b_qkv, out):
 
         transpose_and_quantise(0)
 
-        bias_rows_f32 = keep.tile([P, P], F32)
-        nc.scalar.copy(out=bias_rows_f32[:], in_=bias_rows[:])
         bias_t = psum.tile([P, BANK], F32, tag="kq", bufs=4)
         nc.tensor.transpose(bias_t[:, 0:P], bias_rows_f32[:], ident[:])
         bias = keep.tile([P, 3 * E_TILES], F32)
@@ -452,6 +458,13 @@ def tile_attentionconv_kernel(tc, x, W_qkv_words, W_qkv_scales, b_qkv, out):
         def quad_right(first):
             scale_right(channel, quad(first)[1], first, first + 4, quad(first)[3], True)
 
+        def store_half(half):
+            for b in range(BATCH):
+                nc.sync.dma_start(
+                    out=out[b, channel].rearrange("(m r) w -> m r w", r=PATCH // 2)[:, :, half * WIDTH // 2 : (half + 1) * WIDTH // 2],
+                    in_=image_rows[b : P : BATCH, :, half * J_BANK : (half + 1) * J_BANK, :].rearrange("p r j s -> p r (j s)"),
+                )
+
         sums = {}
 
         def quad_sum(first):
@@ -496,6 +509,7 @@ def tile_attentionconv_kernel(tc, x, W_qkv_words, W_qkv_scales, b_qkv, out):
         fetch_q(q_12, 12)
         quad_multiply(0)
         quad_multiply(4)
+        store_half(0)
         quad_multiply(8)
         quad_multiply(12)
-        nc.sync.dma_start(out=out_rows[channel], in_=image_rows[:].rearrange("p r j s -> p (r j s)"))
+        store_half(1)

@@ -63,15 +63,20 @@ def tile_attentionconv_kernel(tc, x, W_qkv_words, W_qkv_scales, b_qkv, out):
                 in_=W_qkv_scales[:, 4 * quad : 4 * quad + 4, :].bitcast(F32),
             )
 
-        w_words = keep.tile([P, PASSES, 3 * D], U32, align_bytes=64)
-        for first_column, last_column in ((0, D // CHANNELS), (D // CHANNELS, D)):
+        w_words = W_qkv_words.rearrange("g p n t -> p g (n t)")
+
+        def load_words(tile, first_channel, end_channel, in_front):
+            columns = (end_channel - first_channel) * D // CHANNELS
+            width = tile.shape[2] // 3
             for section in (1, 2, 0):
+                first = section * D + first_channel * D // CHANNELS
                 nc.sync.dma_start(
-                    out=w_words[:, :, section * D + first_column : section * D + last_column].bitcast(I32),
-                    in_=W_qkv_words.rearrange("g p n t -> p g (n t)")[
-                        :, :, 4 * (section * D + first_column) : 4 * (section * D + last_column)
-                    ].bitcast(I32),
+                    out=tile[:, :, section * width + in_front : section * width + in_front + columns].bitcast(I32),
+                    in_=w_words[:, :, 4 * first : 4 * (first + columns)].bitcast(I32),
                 )
+
+        w_first = keep.tile([P, PASSES, 3 * D // CHANNELS], U32, align_bytes=64)
+        load_words(w_first, 0, 1, 0)
 
         rs_int = keep.tile([P, 2], I32)
         nc.vector.tensor_single_scalar(out=rs_int[:, 0:1], in_=p_index[:], scalar=PATCH - 1, op=ALU.bitwise_and)
@@ -91,7 +96,7 @@ def tile_attentionconv_kernel(tc, x, W_qkv_words, W_qkv_scales, b_qkv, out):
 
         bias_rows_f32 = keep.tile([P, P], F32)
         x_words = x_sb[:].bitcast(F32).rearrange("p q (r j s u) -> p q u j r s", j=GRID, s=4, u=2)
-        sorted_words = keep.tile([P, GRID, 2, P], F32)
+        sorted_words = keep.tile([P, GRID, 2, P], F32, tag="early", align_bytes=64)
         for quarter in range(QUARTERS):
             shares = ((nc.vector.tensor_copy, 0, GRID),)
             if quarter == QUARTERS - 1:
@@ -160,13 +165,19 @@ def tile_attentionconv_kernel(tc, x, W_qkv_words, W_qkv_scales, b_qkv, out):
 
         transpose_and_quantise(1)
 
+        w_rest = keep.tile([P, PASSES, 3 * D * (CHANNELS - 1) // CHANNELS], U32, tag="early", align_bytes=64)
+        load_words(w_rest, 1, 2, 0)
+        load_words(w_rest, 2, CHANNELS, D // CHANNELS)
+
         def project_tile(tag, bufs, section, channel, half, upper):
             acc = psum.tile([P, BANK], F32, tag=tag, bufs=bufs)
             first = section * D + (2 * channel + upper) * P
+            words = w_rest if channel else w_first
+            place = section * words.shape[2] // 3 + (2 * max(channel - 1, 0) + upper) * P
             for g in range(PASSES):
                 nc.tensor.matmul_mx(
                     out=acc[:],
-                    lhsT=w_words[:, g, first : first + P].bitcast(FP8X4),
+                    lhsT=words[:, g, place : place + P].bitcast(FP8X4),
                     lhsT_scale=w_scales[4 * g : P, first : first + P],
                     rhs=x_codes[:, g, half * BANK : (half + 1) * BANK].bitcast(FP8X4),
                     rhs_scale=x_scales[:, g, half * BANK : (half + 1) * BANK],

@@ -112,10 +112,13 @@ def tile_attentionconv_kernel(tc, x, W_qkv_words, W_qkv_scales, b_qkv, out):
 
         nc.scalar.copy(out=bias_rows_f32[:], in_=bias_rows[:])
 
+        def keep_clock(bank, quarter, repeats):
+            for repeat in range(repeats):
+                nc.tensor.matmul(bank, lhsT=x_sb[:, quarter, 0:P], rhs=x_sb[:, quarter, 0:BANK], start=True, stop=True)
+
         warm = psum.tile([P, BANK], F32, tag="kq", bufs=4)
         for quarter, repeats in ((0, 3), (1, 3), (2, 2)):
-            for repeat in range(repeats):
-                nc.tensor.matmul(warm[:], lhsT=x_sb[:, quarter, 0:P], rhs=x_sb[:, quarter, 0:BANK], start=True, stop=True)
+            keep_clock(warm[:], quarter, repeats)
 
         grouped = keep.tile([P, PASSES, 4 * PATCHES], BF16, align_bytes=64)
         grouped_words = grouped[:].bitcast(F32)
@@ -128,6 +131,8 @@ def tile_attentionconv_kernel(tc, x, W_qkv_words, W_qkv_scales, b_qkv, out):
                     x_t = psum.tile([P, 2, 2 * P], F32, tag=("v" if (j0 // 4) % 2 == 0 else "sum"), bufs=2)
                 else:
                     x_t = psum.tile([P, 2, 2 * P], F32, tag="kq", bufs=4)
+                if j0 % 8 == 0 and j0 > 0:
+                    keep_clock(x_t[:].rearrange("p u n -> p (u n)"), 0, 2)
                 for u in range(2):
                     for jl in range(2):
                         nc.tensor.transpose(x_t[:, u, jl * P : (jl + 1) * P], sorted_words[:, j0 + jl, u, :], ident[:])
@@ -337,10 +342,7 @@ def tile_attentionconv_kernel(tc, x, W_qkv_words, W_qkv_scales, b_qkv, out):
         def sum_columns(channel, tag, from_left, from_right, first, base, warm_ups=0):
             rows_pad = rows_pads[channel]
             sum_t = psum.tile([P, 4, P], F32, tag=tag, bufs=2)
-            for repeat in range(warm_ups):
-                nc.tensor.matmul(
-                    sum_t[:].rearrange("p j n -> p (j n)"), lhsT=x_sb[:, 0, 0:P], rhs=x_sb[:, 0, 0:BANK], start=True, stop=True
-                )
+            keep_clock(sum_t[:].rearrange("p j n -> p (j n)"), 0, warm_ups)
             for j in range(first, first + 4):
                 columns = sum_t[:, j - first, :]
                 nc.tensor.matmul(columns, lhsT=from_left[:, j - base, :], rhs=ident[:], start=True, stop=False, is_transpose=True)
@@ -399,7 +401,7 @@ def tile_attentionconv_kernel(tc, x, W_qkv_words, W_qkv_scales, b_qkv, out):
                 nc.sync.dma_start(out=out_rows[channel - 1], in_=waiting[1][:].rearrange("p r j s -> p (r j s)"))
             sums = []
             for first in range(0, J_BANK, 4):
-                sums.append(sum_columns(channel, "sum", from_left, from_right, first, 0, 0))
+                sums.append(sum_columns(channel, "sum", from_left, from_right, first, 0, 2 if first == 0 else 0))
 
             borders(after, kv_pads[after], rows_pads[after])
 
@@ -480,7 +482,7 @@ def tile_attentionconv_kernel(tc, x, W_qkv_words, W_qkv_scales, b_qkv, out):
 
         def quad_sum(first):
             from_left, from_right, q_t_sb, base = quad(first)
-            sums[first] = sum_columns(channel, ("sum", "v")[first // J_BANK], from_left, from_right, first, base)
+            sums[first] = sum_columns(channel, ("sum", "v")[first // J_BANK], from_left, from_right, first, base, 2 if first == 0 else 0)
 
         def quad_multiply(first):
             multiply_q(sums[first], quad(first)[2], image_rows, first, quad(first)[3])

@@ -55,7 +55,7 @@ def tile_attentionconv_kernel(tc, x, W_qkv_words, W_qkv_scales, b_qkv, out):
         nc.vector.memset(bias_rows[:], 0.0)
         nc.gpsimd.dma_start(out=bias_rows[0 : 3 * E_TILES, :], in_=b_qkv.rearrange("(t p) -> t p", p=P))
 
-        w_scales = keep.tile([P, 3 * D], U8, align_bytes=64)
+        w_scales = keep.tile([P, 3 * D], U8, align_bytes=256)
         nc.vector.memset(w_scales[:].bitcast(I32), 0)
         for quad in range(4):
             nc.gpsimd.dma_start(
@@ -75,7 +75,7 @@ def tile_attentionconv_kernel(tc, x, W_qkv_words, W_qkv_scales, b_qkv, out):
                     in_=w_words[:, :, 4 * first : 4 * (first + columns)].bitcast(I32),
                 )
 
-        w_first = keep.tile([P, PASSES, 3 * D // CHANNELS], U32, align_bytes=64)
+        w_first = keep.tile([P, PASSES, 3 * D // CHANNELS], U32, align_bytes=256)
         load_words(w_first, 0, 1, 0)
 
         rs_int = keep.tile([P, 2], I32)
@@ -96,7 +96,7 @@ def tile_attentionconv_kernel(tc, x, W_qkv_words, W_qkv_scales, b_qkv, out):
 
         bias_rows_f32 = keep.tile([P, P], F32)
         x_words = x_sb[:].bitcast(F32).rearrange("p q (r j s u) -> p q u j r s", j=GRID, s=4, u=2)
-        sorted_words = keep.tile([P, GRID, 2, P], F32, tag="early", align_bytes=64)
+        sorted_words = keep.tile([P, GRID, 2, P], F32, tag="early", align_bytes=256)
         for quarter in range(QUARTERS):
             shares = ((nc.vector.tensor_copy, 0, GRID),)
             if quarter == QUARTERS - 1:
@@ -122,8 +122,8 @@ def tile_attentionconv_kernel(tc, x, W_qkv_words, W_qkv_scales, b_qkv, out):
 
         grouped = keep.tile([P, PASSES, 4 * PATCHES], BF16, align_bytes=64)
         grouped_words = grouped[:].bitcast(F32)
-        x_codes = keep.tile([P, PASSES, PATCHES], U32, align_bytes=64)
-        x_scales = keep.tile([P, PASSES, PATCHES], U8, align_bytes=64)
+        x_codes = keep.tile([P, PASSES, PATCHES], U32, align_bytes=256)
+        x_scales = keep.tile([P, PASSES, PATCHES], U8, align_bytes=256)
         def transpose_and_quantise(half):
             for j0 in range(half * J_BANK, (half + 1) * J_BANK, 2):
                 odd = (j0 // 2) % 2 and j0 != 10
@@ -170,7 +170,7 @@ def tile_attentionconv_kernel(tc, x, W_qkv_words, W_qkv_scales, b_qkv, out):
 
         transpose_and_quantise(1)
 
-        w_rest = keep.tile([P, PASSES, 3 * D * (CHANNELS - 1) // CHANNELS], U32, tag="early", align_bytes=64)
+        w_rest = keep.tile([P, PASSES, 3 * D * (CHANNELS - 1) // CHANNELS], U32, tag="early", align_bytes=256)
         load_words(w_rest, 1, 2, 0)
         load_words(w_rest, 2, CHANNELS, D // CHANNELS)
 
@@ -385,7 +385,8 @@ def tile_attentionconv_kernel(tc, x, W_qkv_words, W_qkv_scales, b_qkv, out):
                 for upper in range(2):
                     sum_rows(channel, J_BANK, GRID, step, upper)
             from_right = work.tile([P, J_BANK, P], F32, tag="from_right")
-            scale_right(channel, from_right, 0, J_BANK, 0, True)
+            scale_right(channel, from_right, 0, J_BANK - 1, 0, True)
+            scale_right(channel, from_right, J_BANK - 1, J_BANK, 0, True)
 
             start_channel(after)
             project_k(after, 0, k_sbs[after])
@@ -460,10 +461,9 @@ def tile_attentionconv_kernel(tc, x, W_qkv_words, W_qkv_scales, b_qkv, out):
         def fetch_q(q_t, first):
             nc.scalar.copy(out=quad(first)[2][:, first - quad(first)[3] : first - quad(first)[3] + 4, :], in_=q_t[:])
 
-        def rows(first, end):
-            for step in range(2):
-                for upper in range(2):
-                    sum_rows(channel, first, end, step, upper)
+        def rows(first, end, step):
+            for upper in range(2):
+                sum_rows(channel, first, end, step, upper)
 
         def quad_left(first):
             scale_left(channel, quad(first)[0], first, first + 4, quad(first)[3])
@@ -493,34 +493,38 @@ def tile_attentionconv_kernel(tc, x, W_qkv_words, W_qkv_scales, b_qkv, out):
         right_4 = transpose_right(waiting[0], 4)
         q_0 = transpose_q(channel, 0)
         q_4 = transpose_q(channel, 4)
-        rows(0, 5)
+        rows(0, 5, 0)
+        rows(0, 5, 1)
         quad_left(0)
+        rows(5, J_BANK, 0)
         quad_right(0)
         quad_sum(0)
+        rows(5, J_BANK, 1)
         fetch_right(right_0, waiting[1], 0)
         fetch_right(right_4, waiting[1], 4)
         nc.sync.dma_start(out=out_rows[channel - 1], in_=waiting[1][:].rearrange("p r j s -> p (r j s)"))
-        rows(5, J_BANK)
         quad_left(4)
         q_8 = transpose_q(channel, 8)
         for upper in range(2):
             multiply_kv(channel, 1, upper, v_banks[channel, 1], k_sbs[channel], kv_pads[channel])
-        rows(J_BANK, 13)
-        quad_right(4)
-        quad_right(8)
+        rows(J_BANK, 13, 0)
+        rows(J_BANK, 13, 1)
         quad_left(8)
+        rows(13, GRID, 0)
+        quad_right(4)
         quad_sum(4)
+        quad_right(8)
         quad_sum(8)
         fetch_q(q_0, 0)
-        rows(13, GRID)
-        quad_right(12)
+        rows(13, GRID, 1)
         quad_left(12)
         q_12 = transpose_q(channel, 12)
-        quad_sum(12)
         fetch_q(q_4, 4)
+        quad_multiply(0)
+        quad_right(12)
+        quad_sum(12)
         fetch_q(q_8, 8)
         fetch_q(q_12, 12)
-        quad_multiply(0)
         quad_multiply(4)
         store_half(0)
         quad_multiply(8)

@@ -120,7 +120,7 @@ def tile_attentionconv_kernel(tc, x, W_qkv_words, W_qkv_scales, b_qkv, out):
         for quarter, repeats in ((0, 3), (1, 3), (2, 2)):
             keep_clock(warm[:], quarter, repeats)
 
-        grouped = keep.tile([P, PASSES, 4 * PATCHES], BF16, align_bytes=64)
+        grouped = keep.tile([P, HALVES, PASSES, 4 * BANK], BF16, align_bytes=64)
         grouped_words = grouped[:].bitcast(F32)
         x_codes = keep.tile([P, PASSES, PATCHES], U32, align_bytes=256)
         x_scales = keep.tile([P, PASSES, PATCHES], U8, align_bytes=256)
@@ -137,15 +137,16 @@ def tile_attentionconv_kernel(tc, x, W_qkv_words, W_qkv_scales, b_qkv, out):
                     for jl in range(2):
                         nc.tensor.transpose(x_t[:, u, jl * P : (jl + 1) * P], sorted_words[:, j0 + jl, u, :], ident[:])
                 copy = nc.vector.tensor_copy if odd else nc.scalar.copy
+                place = (j0 - half * J_BANK) * 2 * COLUMN
                 copy(
-                    out=grouped_words[:, :, j0 * 2 * COLUMN : (j0 + 2) * 2 * COLUMN].rearrange("p g (m u) -> p g m u", u=2),
+                    out=grouped_words[:, half, :, place : place + 4 * COLUMN].rearrange("p g (m u) -> p g m u", u=2),
                     in_=x_t[:].rearrange("p u (m g) -> p g m u", g=PASSES),
                 )
             for g in range(PASSES):
                 nc.vector.quantize_mx(
                     out=x_codes[:, g, half * BANK : (half + 1) * BANK].bitcast(FP8X4),
                     scales=x_scales[:, g, half * BANK : (half + 1) * BANK],
-                    in_=grouped[:, g, 4 * half * BANK : 4 * (half + 1) * BANK],
+                    in_=grouped[:, half, g, :],
                 )
 
         transpose_and_quantise(0)

@@ -391,6 +391,7 @@ def tile_attentionconv_kernel(tc, x, W_qkv_words, W_qkv_scales, b_qkv, out):
 
             start_channel(after)
             project_k(after, 0, k_sbs[after])
+            borders(after, kv_pads[after], rows_pads[after])
             v_banks[after, 0] = project("v", 2, 2, after, 0)
 
             q_t_sb = work.tile([P, J_BANK, P], F32, tag="q_t_sb")
@@ -404,8 +405,6 @@ def tile_attentionconv_kernel(tc, x, W_qkv_words, W_qkv_scales, b_qkv, out):
             sums = []
             for first in range(0, J_BANK, 4):
                 sums.append(sum_columns(channel, "sum", from_left, from_right, first, 0, 2 if first == 0 else 0))
-
-            borders(after, kv_pads[after], rows_pads[after])
 
             window = work.tile([P, J_BANK, P], F32, tag="window")
             for j0 in range(0, J_BANK, 4):

from contextlib import ExitStack

import concourse.mybir as mybir
from concourse.masks import make_identity

F32 = mybir.dt.float32
BF16 = mybir.dt.bfloat16
I32 = mybir.dt.int32
U32 = mybir.dt.uint32
U8 = mybir.dt.uint8
FP8X4 = mybir.dt.float8_e4m3fn_x4
ALU = mybir.AluOpType
ACT = mybir.ActivationFunctionType

P = 128
BATCH = 4
CHANNELS = 4
PATCH = 16
GRID = 16
WIDTH = GRID * PATCH
D = CHANNELS * PATCH * PATCH
PATCHES = BATCH * GRID * GRID
K_PASS = 4 * P
PASSES = D // K_PASS
BANK = 512
HALVES = PATCHES // BANK
COLUMN = GRID * BATCH
J_BANK = BANK // COLUMN
E_TILES = D // P
QUARTERS = 4
PAD = 8

FLOPS = 2 * PATCHES * D * 3 * D


def tile_attentionconv_kernel(tc, x, W_qkv_words, W_qkv_scales, b_qkv, out):
    nc = tc.nc
    with ExitStack() as ctx:
        ctx.enter_context(tc.manual_schedule())
        keep = ctx.enter_context(tc.tile_pool(name="keep", bufs=1))
        work = ctx.enter_context(tc.tile_pool(name="work", bufs=2))
        psum = ctx.enter_context(tc.psum_pool(name="psum", bufs=4))

        p_index = keep.tile([P, 1], I32)
        nc.gpsimd.iota(p_index[:], pattern=[[0, 1]], base=0, channel_multiplier=1)
        ident = keep.tile([P, P], F32)
        make_identity(nc, ident[:])

        x_rows = x.rearrange("b (g c) (i q r) w -> c q i (b g) (r w)", g=2, c=2, i=GRID, q=2)
        x_sb = keep.tile([P, QUARTERS, PATCH // 2 * WIDTH], BF16)
        for quarter in range(QUARTERS):
            nc.sync.dma_start(out=x_sb[:, quarter, :], in_=x_rows[quarter // 2, quarter % 2])

        bias_rows = keep.tile([P, P], BF16)
        nc.vector.memset(bias_rows[:], 0.0)
        nc.gpsimd.dma_start(out=bias_rows[0 : 3 * E_TILES, :], in_=b_qkv.rearrange("(t p) -> t p", p=P))

        w_scales = keep.tile([P, 3 * D], U8, align_bytes=256)
        nc.vector.memset(w_scales[:].bitcast(I32), 0)
        for quad in range(4):
            nc.gpsimd.dma_start(
                out=w_scales[32 * quad : 32 * quad + 4 * PASSES, :].bitcast(F32),
                in_=W_qkv_scales[:, 4 * quad : 4 * quad + 4, :].bitcast(F32),
            )

        w_words = W_qkv_words.rearrange("g p n t -> p g (n t)")

        def load_words(tile, first_channel, end_channel, in_front):
            columns = (end_channel - first_channel) * D // CHANNELS
            width = tile.shape[2] // 3
            for section in (1, 2, 0):
                first = section * D + first_channel * D // CHANNELS
                nc.sync.dma_start(
                    out=tile[:, :, section * width + in_front : section * width + in_front + columns].bitcast(I32),
                    in_=w_words[:, :, 4 * first : 4 * (first + columns)].bitcast(I32),
                )

        w_first = keep.tile([P, PASSES, 3 * D // CHANNELS], U32, align_bytes=256)
        load_words(w_first, 0, 1, 0)

        rs_int = keep.tile([P, 2], I32)
        nc.vector.tensor_single_scalar(out=rs_int[:, 0:1], in_=p_index[:], scalar=PATCH - 1, op=ALU.bitwise_and)
        nc.vector.tensor_single_scalar(out=rs_int[:, 1:2], in_=p_index[:], scalar=4, op=ALU.logical_shift_right)
        rs = keep.tile([P, 2], F32)
        nc.vector.tensor_copy(out=rs[:], in_=rs_int[:])
        s_col = rs[:, 0:1]
        r_col = rs[:, 1:2]
        exponents = keep.tile([P, 6], F32)
        nc.vector.tensor_scalar(out=exponents[:, 0:1], in0=s_col, scalar1=0.125, scalar2=-15.0 / 8.0, op0=ALU.mult, op1=ALU.add)
        nc.vector.tensor_scalar(out=exponents[:, 1:2], in0=s_col, scalar1=-0.125, scalar2=0.0, op0=ALU.mult, op1=ALU.add)
        for upper in range(2):
            nc.vector.tensor_scalar(out=exponents[:, 2 + upper : 3 + upper], in0=r_col, scalar1=0.125, scalar2=(8.0 * upper - 15.0) / 8.0, op0=ALU.mult, op1=ALU.add)
            nc.vector.tensor_scalar(out=exponents[:, 4 + upper : 5 + upper], in0=r_col, scalar1=-0.125, scalar2=-1.0 * upper, op0=ALU.mult, op1=ALU.add)
        taps = keep.tile([P, 6], F32)
        nc.scalar.activation(out=taps[:], in_=exponents[:], func=ACT.Exp)

        bias_rows_f32 = keep.tile([P, P], F32)
        x_words = x_sb[:].bitcast(F32).rearrange("p q (r j s u) -> p q u j r s", j=GRID, s=4, u=2)
        sorted_words = keep.tile([P, GRID, 2, P], F32, tag="early", align_bytes=256)
        for quarter in range(QUARTERS):
            shares = ((nc.vector.tensor_copy, 0, GRID),)
            if quarter == QUARTERS - 1:
                shares = ((nc.vector.tensor_copy, 0, J_BANK), (nc.scalar.copy, J_BANK, GRID))
            for copy, first, end in shares:
                for u in range(2):
                    copy(
                        out=sorted_words[:, first:end, u, quarter * P // QUARTERS : (quarter + 1) * P // QUARTERS].rearrange(
                            "p j (r s) -> p j r s", s=4
                        ),
                        in_=x_words[:, quarter, u, first:end],
                    )

        nc.scalar.copy(out=bias_rows_f32[:], in_=bias_rows[:])

        def keep_clock(bank, quarter, repeats):
            for repeat in range(repeats):
                nc.tensor.matmul(bank, lhsT=x_sb[:, quarter, 0:P], rhs=x_sb[:, quarter, 0:BANK], start=True, stop=True)

        warm = psum.tile([P, BANK], F32, tag="kq", bufs=4)
        for quarter, repeats in ((0, 3), (1, 3), (2, 2)):
            keep_clock(warm[:], quarter, repeats)

        grouped = keep.tile([P, HALVES, PASSES, 4 * BANK], BF16, align_bytes=64)
        grouped_words = grouped[:].bitcast(F32)
        x_codes = keep.tile([P, PASSES, PATCHES], U32, align_bytes=256)
        x_scales = keep.tile([P, PASSES, PATCHES], U8, align_bytes=256)
        def transpose_and_quantise(half):
            for j0 in range(half * J_BANK, (half + 1) * J_BANK, 2):
                odd = (j0 // 2) % 2 and j0 != 10
                if odd:
                    x_t = psum.tile([P, 2, 2 * P], F32, tag=("v" if (j0 // 4) % 2 == 0 else "sum"), bufs=2)
                else:
                    x_t = psum.tile([P, 2, 2 * P], F32, tag="kq", bufs=4)
                if j0 % 8 == 0 and j0 > 0:
                    keep_clock(x_t[:].rearrange("p u n -> p (u n)"), 0, 2)
                for u in range(2):
                    for jl in range(2):
                        nc.tensor.transpose(x_t[:, u, jl * P : (jl + 1) * P], sorted_words[:, j0 + jl, u, :], ident[:])
                copy = nc.vector.tensor_copy if odd else nc.scalar.copy
                place = (j0 - half * J_BANK) * 2 * COLUMN
                copy(
                    out=grouped_words[:, half, :, place : place + 4 * COLUMN].rearrange("p g (m u) -> p g m u", u=2),
                    in_=x_t[:].rearrange("p u (m g) -> p g m u", g=PASSES),
                )
            for g in range(PASSES):
                nc.vector.quantize_mx(
                    out=x_codes[:, g, half * BANK : (half + 1) * BANK].bitcast(FP8X4),
                    scales=x_scales[:, g, half * BANK : (half + 1) * BANK],
                    in_=grouped[:, half, g, :],
                )

        transpose_and_quantise(0)

        bias_t = psum.tile([P, BANK], F32, tag="kq", bufs=4)
        nc.tensor.transpose(bias_t[:, 0:P], bias_rows_f32[:], ident[:])
        bias = keep.tile([P, 3 * E_TILES], F32)
        nc.scalar.copy(out=bias[:], in_=bias_t[:, 0 : 3 * E_TILES])

        edge = keep.tile([P, E_TILES], F32)
        nc.gpsimd.tensor_tensor(out=edge[:], in0=bias[:, E_TILES : 2 * E_TILES], in1=bias[:, 2 * E_TILES : 3 * E_TILES], op=ALU.mult)
        tap_sum = keep.tile([P, 2], F32)
        nc.gpsimd.tensor_tensor(out=tap_sum[:], in0=taps[:, 2:4], in1=taps[:, 4:6], op=ALU.add)
        nc.gpsimd.tensor_scalar_add(out=tap_sum[:], in0=tap_sum[:], scalar1=1.0)
        edge_rows = keep.tile([P, E_TILES], F32)
        nc.gpsimd.tensor_tensor(
            out=edge_rows[:].rearrange("p (c h) -> p c h", h=2),
            in0=edge[:].rearrange("p (c h) -> p c h", h=2),
            in1=tap_sum[:].unsqueeze(1).to_broadcast([P, CHANNELS, 2]),
            op=ALU.mult,
        )

        transpose_and_quantise(1)

        w_rest = keep.tile([P, PASSES, 3 * D * (CHANNELS - 1) // CHANNELS], U32, tag="early", align_bytes=256)
        load_words(w_rest, 1, 2, 0)
        load_words(w_rest, 2, CHANNELS, D // CHANNELS)

        def project_tile(tag, bufs, section, channel, half, upper):
            acc = psum.tile([P, BANK], F32, tag=tag, bufs=bufs)
            first = section * D + (2 * channel + upper) * P
            words = w_rest if channel else w_first
            place = section * words.shape[2] // 3 + (2 * max(channel - 1, 0) + upper) * P
            for g in range(PASSES):
                nc.tensor.matmul_mx(
                    out=acc[:],
                    lhsT=words[:, g, place : place + P].bitcast(FP8X4),
                    lhsT_scale=w_scales[4 * g : P, first : first + P],
                    rhs=x_codes[:, g, half * BANK : (half + 1) * BANK].bitcast(FP8X4),
                    rhs_scale=x_scales[:, g, half * BANK : (half + 1) * BANK],
                    start=(g == 0),
                    stop=(g == PASSES - 1),
                )
            return acc

        def project(tag, bufs, section, channel, half):
            lower_tile = project_tile(tag, bufs, section, channel, half, 0)
            upper_tile = project_tile(tag, bufs, section, channel, half, 1)
            return [lower_tile, upper_tile]

        def project_kv(channel, half, tag):
            v_tiles = []
            for upper in range(2):
                k_ps = project_tile("kq", 4, 1, channel, half, upper)
                nc.scalar.activation(
                    out=k_sbs[channel][:, upper, half * BANK : (half + 1) * BANK],
                    in_=k_ps[:],
                    func=ACT.Identity,
                    bias=bias_of(1, channel, upper),
                    scale=1.0,
                )
                v_tile = project_tile(tag, 2, 2, channel, half, upper)
                v_tiles.append(v_tile)
            v_banks[channel, half] = v_tiles

        def bias_of(section, channel, upper):
            column = section * E_TILES + 2 * channel + upper
            return bias[:, column : column + 1]

        def project_k(channel, half, k_sb):
            k_ps = project("kq", 4, 1, channel, half)
            for upper in range(2):
                nc.scalar.activation(
                    out=k_sb[:, upper, half * BANK : (half + 1) * BANK],
                    in_=k_ps[upper][:],
                    func=ACT.Identity,
                    bias=bias_of(1, channel, upper),
                    scale=1.0,
                )

        def project_q(channel, half, q_sb):
            q_ps = project("kq", 4, 0, channel, half)
            for upper in range(2):
                nc.scalar.activation(
                    out=q_sb[:, half * J_BANK : (half + 1) * J_BANK, :, upper, :],
                    in_=q_ps[upper][:].rearrange("p (j i b) -> p j i b", i=GRID, b=BATCH),
                    func=ACT.Identity,
                    bias=bias_of(0, channel, upper),
                    scale=1.0,
                )

        def borders(channel, kv_pad, rows_pad):
            for upper in range(2):
                et = 2 * channel + upper
                nc.scalar.copy(
                    out=kv_pad[:, upper].rearrange("p j (k w) -> p j k w", w=PAD)[:, :, 0 : COLUMN // PAD + 2 : COLUMN // PAD + 1, :],
                    in_=edge[:, et : et + 1].unsqueeze(2).unsqueeze(3).to_broadcast([P, GRID, 2, PAD]),
                )
                nc.scalar.copy(
                    out=rows_pad[:, 0 : GRID + 2 : GRID + 1, :, upper, :],
                    in_=edge_rows[:, et : et + 1].unsqueeze(2).unsqueeze(3).to_broadcast([P, 2, GRID, BATCH]),
                )

        def multiply_kv(channel, half, upper, v_ps, k_sb, kv_pad):
            nc.vector.scalar_tensor_tensor(
                out=kv_pad[:, upper, half * J_BANK : (half + 1) * J_BANK, PAD : PAD + COLUMN],
                in0=v_ps[upper][:].rearrange("p (j n) -> p j n", n=COLUMN),
                scalar=bias_of(2, channel, upper),
                in1=k_sb[:, upper, half * BANK : (half + 1) * BANK].rearrange("p (j n) -> p j n", n=COLUMN),
                op0=ALU.add,
                op1=ALU.mult,
            )

        def flat(columns):
            return columns.rearrange("p j i h b -> p (j i h b)")

        out_rows = out.rearrange("b c (m r) w -> c m b (r w)", r=PATCH // 2)


        k_sbs = {}
        v_banks = {}
        kv_pads = {}
        rows_pads = {}
        q_sbs = {}

        def start_channel(channel):
            k_sb = work.tile([P, 2, PATCHES], F32, tag="k_sb")
            kv_pad = work.tile([P, 2, GRID, PAD + COLUMN + PAD], F32, tag="kv_pad")
            rows_pad = work.tile([P, GRID + 2, GRID, 2, BATCH], F32, tag="rows_pad")
            k_sbs[channel] = k_sb
            kv_pads[channel] = kv_pad
            rows_pads[channel] = rows_pad

        start_channel(0)
        project_k(0, 0, k_sbs[0])
        borders(0, kv_pads[0], rows_pads[0])
        v_banks[0, 0] = project("v", 2, 2, 0, 0)
        project_k(0, 1, k_sbs[0])
        v_banks[0, 1] = project("sum", 2, 2, 0, 1)
        for upper in range(2):
            multiply_kv(0, 0, upper, v_banks[0, 0], k_sbs[0], kv_pads[0])

        def sum_rows(channel, first, end, step, upper):
            kv_pad = kv_pads[channel]
            rows_pad = rows_pads[channel]
            shift = (PAD - BATCH, PAD + BATCH)[step]
            nc.vector.scalar_tensor_tensor(
                out=rows_pad[:, first + 1 : end + 1, :, upper, :],
                in0=kv_pad[:, upper, first:end, shift : shift + COLUMN].rearrange("p j (i b) -> p j i b", b=BATCH),
                scalar=taps[:, 2 + 2 * step + upper : 3 + 2 * step + upper],
                in1=(
                    kv_pad[:, upper, first:end, PAD : PAD + COLUMN].rearrange("p j (i b) -> p j i b", b=BATCH)
                    if step == 0
                    else rows_pad[:, first + 1 : end + 1, :, upper, :]
                ),
                op0=ALU.mult,
                op1=ALU.add,
            )

        def scale_left(channel, scaled, first, end, base):
            nc.scalar.activation(
                out=scaled[:, first - base : end - base, :].rearrange("p j n -> p (j n)"),
                in_=flat(rows_pads[channel][:, first:end]),
                func=ACT.Identity,
                scale=taps[:, 0:1],
            )

        def scale_right(channel, scaled, first, end, base, on_vector):
            target = scaled[:, first - base : end - base, :].rearrange("p j n -> p (j n)")
            source = flat(rows_pads[channel][:, first + 2 : end + 2])
            if on_vector:
                nc.vector.tensor_scalar_mul(out=target, in0=source, scalar1=taps[:, 1:2])
            else:
                nc.scalar.activation(out=target, in_=source, func=ACT.Identity, scale=taps[:, 1:2])

        def transpose_q(channel, first):
            q_t = psum.tile([P, 4, P], F32, tag="kq", bufs=4)
            for jl in range(4):
                nc.tensor.transpose(q_t[:, jl, :], q_sbs[channel][:, first + jl].rearrange("p i h b -> p (i h b)"), ident[:])
            return q_t

        def transpose_right(result, j0):
            out_t = psum.tile([P, 4, P], F32, tag="kq", bufs=4)
            for jl in range(4):
                nc.tensor.transpose(out_t[:, jl, :], result[:, j0 + jl, :], ident[:])
            return out_t

        def fetch_right(out_t, image_rows, j0):
            nc.scalar.copy(
                out=image_rows[:, :, J_BANK + j0 : J_BANK + j0 + 4, :],
                in_=out_t[:].rearrange("p j (r s) -> p r j s", s=PATCH),
            )

        def sum_columns(channel, tag, from_left, from_right, first, base, warm_ups=0):
            rows_pad = rows_pads[channel]
            sum_t = psum.tile([P, 4, P], F32, tag=tag, bufs=2)
            keep_clock(sum_t[:].rearrange("p j n -> p (j n)"), 0, warm_ups)
            for j in range(first, first + 4):
                columns = sum_t[:, j - first, :]
                nc.tensor.matmul(columns, lhsT=from_left[:, j - base, :], rhs=ident[:], start=True, stop=False, is_transpose=True)
                nc.tensor.matmul(
                    columns,
                    lhsT=rows_pad[:, j + 1].rearrange("p i h b -> p (i h b)"),
                    rhs=ident[:],
                    start=False,
                    stop=False,
                    is_transpose=True,
                )
                nc.tensor.matmul(columns, lhsT=from_right[:, j - base, :], rhs=ident[:], start=False, stop=True, is_transpose=True)
            return sum_t

        def multiply_q(sum_t, q_t_sb, image_rows, first, base):
            nc.vector.tensor_tensor(
                out=image_rows[:, :, first : first + 4, :],
                in0=sum_t[:].rearrange("p j (r s) -> p r j s", s=PATCH),
                in1=q_t_sb[:, first - base : first - base + 4, :].rearrange("p j (r s) -> p r j s", s=PATCH),
                op=ALU.mult,
            )

        waiting = None
        for channel in range(CHANNELS - 1):
            after = channel + 1
            rows_pad = rows_pads[channel]
            q_sb = work.tile([P, GRID, GRID, 2, BATCH], F32, tag="q_sb")
            q_sbs[channel] = q_sb
            for half in range(HALVES):
                project_q(channel, half, q_sb)

            for step in range(2):
                for upper in range(2):
                    sum_rows(channel, 0, J_BANK, step, upper)
            from_left = work.tile([P, J_BANK, P], F32, tag="from_left")
            scale_left(channel, from_left, 0, J_BANK, 0)
            for upper in range(2):
                multiply_kv(channel, 1, upper, v_banks[channel, 1], k_sbs[channel], kv_pads[channel])
            for step in range(2):
                for upper in range(2):
                    sum_rows(channel, J_BANK, GRID, step, upper)
            from_right = work.tile([P, J_BANK, P], F32, tag="from_right")
            scale_right(channel, from_right, 0, J_BANK - 1, 0, True)
            scale_right(channel, from_right, J_BANK - 1, J_BANK, 0, True)

            start_channel(after)
            project_k(after, 0, k_sbs[after])
            borders(after, kv_pads[after], rows_pads[after])
            v_banks[after, 0] = project("v", 2, 2, after, 0)

            q_t_sb = work.tile([P, J_BANK, P], F32, tag="q_t_sb")
            for first in range(0, J_BANK, 4):
                q_t = transpose_q(channel, first)
                nc.scalar.copy(out=q_t_sb[:, first : first + 4, :], in_=q_t[:])
            if waiting is not None:
                for j0 in range(0, J_BANK, 4):
                    fetch_right(transpose_right(waiting[0], j0), waiting[1], j0)
                nc.sync.dma_start(out=out_rows[channel - 1], in_=waiting[1][:].rearrange("p r j s -> p (r j s)"))
            sums = []
            for first in range(0, J_BANK, 4):
                sums.append(sum_columns(channel, "sum", from_left, from_right, first, 0, 2 if first == 0 else 0))

            window = work.tile([P, J_BANK, P], F32, tag="window")
            for j0 in range(0, J_BANK, 4):
                nc.vector.scalar_tensor_tensor(
                    out=window[:, j0 : j0 + 4, :].rearrange("p j n -> p (j n)"),
                    in0=flat(rows_pad[:, J_BANK + j0 : J_BANK + j0 + 4]),
                    scalar=taps[:, 0:1],
                    in1=flat(rows_pad[:, J_BANK + j0 + 1 : J_BANK + j0 + 5]),
                    op0=ALU.mult,
                    op1=ALU.add,
                )
            for j0 in range(0, J_BANK, 4):
                nc.vector.scalar_tensor_tensor(
                    out=window[:, j0 : j0 + 4, :].rearrange("p j n -> p (j n)"),
                    in0=flat(rows_pad[:, J_BANK + j0 + 2 : J_BANK + j0 + 6]),
                    scalar=taps[:, 1:2],
                    in1=window[:, j0 : j0 + 4, :].rearrange("p j n -> p (j n)"),
                    op0=ALU.mult,
                    op1=ALU.add,
                )
            result = work.tile([P, J_BANK, P], F32, tag="result")
            for j0 in range(0, J_BANK, 4):
                nc.gpsimd.tensor_tensor(
                    out=result[:, j0 : j0 + 4, :].rearrange("p j n -> p (j n)"),
                    in0=flat(q_sb[:, J_BANK + j0 : J_BANK + j0 + 4]),
                    in1=window[:, j0 : j0 + 4, :].rearrange("p j n -> p (j n)"),
                    op=ALU.mult,
                )

            for upper in range(2):
                multiply_kv(after, 0, upper, v_banks[after, 0], k_sbs[after], kv_pads[after])
            image_rows = work.tile([P, PATCH // 2, GRID, PATCH], F32, tag="image_rows")
            for first in range(0, J_BANK, 4):
                multiply_q(sums[first // 4], q_t_sb, image_rows, first, 0)
            waiting = (result, image_rows)

            project_k(after, 1, k_sbs[after])
            v_banks[after, 1] = project("v", 2, 2, after, 1)

        channel = CHANNELS - 1
        q_sb = work.tile([P, GRID, GRID, 2, BATCH], F32, tag="q_sb")
        q_sbs[channel] = q_sb
        image_rows = work.tile([P, PATCH // 2, GRID, PATCH], F32, tag="image_rows")
        halves = []
        for half in range(HALVES):
            from_left = work.tile([P, J_BANK, P], F32, tag="from_left")
            from_right = work.tile([P, J_BANK, P], F32, tag="from_right")
            q_t_sb = work.tile([P, J_BANK, P], F32, tag="q_t_sb")
            halves.append((from_left, from_right, q_t_sb))

        def quad(first):
            return halves[first // J_BANK] + (first // J_BANK * J_BANK,)

        def fetch_q(q_t, first):
            nc.scalar.copy(out=quad(first)[2][:, first - quad(first)[3] : first - quad(first)[3] + 4, :], in_=q_t[:])

        def rows(first, end, step):
            for upper in range(2):
                sum_rows(channel, first, end, step, upper)

        def quad_left(first):
            scale_left(channel, quad(first)[0], first, first + 4, quad(first)[3])

        def quad_right(first):
            scale_right(channel, quad(first)[1], first, first + 4, quad(first)[3], True)

        def store_half(half):
            for b in range(BATCH):
                nc.sync.dma_start(
                    out=out[b, channel].rearrange("(m r) w -> m r w", r=PATCH // 2)[:, :, half * WIDTH // 2 : (half + 1) * WIDTH // 2],
                    in_=image_rows[b : P : BATCH, :, half * J_BANK : (half + 1) * J_BANK, :].rearrange("p r j s -> p r (j s)"),
                )

        sums = {}

        def quad_sum(first):
            from_left, from_right, q_t_sb, base = quad(first)
            sums[first] = sum_columns(channel, ("sum", "v")[first // J_BANK], from_left, from_right, first, base, 2 if first == 0 else 0)

        def quad_multiply(first):
            multiply_q(sums[first], quad(first)[2], image_rows, first, quad(first)[3])

        for half in range(HALVES):
            project_q(channel, half, q_sb)
        right_0 = transpose_right(waiting[0], 0)
        right_4 = transpose_right(waiting[0], 4)
        q_0 = transpose_q(channel, 0)
        q_4 = transpose_q(channel, 4)
        rows(0, 5, 0)
        rows(0, 5, 1)
        quad_left(0)
        rows(5, J_BANK, 0)
        quad_right(0)
        quad_sum(0)
        rows(5, J_BANK, 1)
        fetch_right(right_0, waiting[1], 0)
        fetch_right(right_4, waiting[1], 4)
        nc.sync.dma_start(out=out_rows[channel - 1], in_=waiting[1][:].rearrange("p r j s -> p (r j s)"))
        quad_left(4)
        q_8 = transpose_q(channel, 8)
        for upper in range(2):
            multiply_kv(channel, 1, upper, v_banks[channel, 1], k_sbs[channel], kv_pads[channel])
        rows(J_BANK, 13, 0)
        rows(J_BANK, 13, 1)
        quad_left(8)
        rows(13, GRID, 0)
        quad_right(4)
        quad_sum(4)
        quad_right(8)
        quad_sum(8)
        fetch_q(q_0, 0)
        rows(13, GRID, 1)
        quad_left(12)
        q_12 = transpose_q(channel, 12)
        fetch_q(q_4, 4)
        quad_multiply(0)
        quad_right(12)
        quad_sum(12)
        fetch_q(q_8, 8)
        fetch_q(q_12, 12)
        quad_multiply(4)
        store_half(0)
        quad_multiply(8)
        quad_multiply(12)
        store_half(1)
